import numpy as np
import ml_dtypes


def mxq(x, axis, fmt="e4m3"):
    dtype, down = {"e4m3": (ml_dtypes.float8_e4m3fn, 7), "e5m2": (ml_dtypes.float8_e5m2, 14)}[fmt]
    v = np.moveaxis(np.asarray(x, np.float32).astype(ml_dtypes.bfloat16).astype(np.float64), axis, -1)
    blocks = v.reshape(v.shape[:-1] + (-1, 32))
    amax = np.abs(blocks).max(-1, keepdims=True)
    byte = np.maximum(np.where(amax > 0, np.frexp(amax)[1] - 1 + 127, 0) - down, 1)
    scale = np.exp2(byte - 127.0)
    codes = (blocks / scale).astype(np.float32).astype(dtype).astype(np.float64)
    return np.moveaxis((codes * scale).reshape(v.shape), -1, axis)


WIDE = False


def mx_kscale(k):
    if not WIDE:
        return np.ones(k)
    levels = np.array([10, -10, 5, -5, 0])
    if k % 512:
        return np.exp2(np.random.permutation(np.resize(levels, k // 32))).repeat(32)
    a = np.empty((k // 512, 16))
    for p in range(k // 512):
        a[p, :8] = np.random.permutation(np.resize(levels, 8))
        for g in range(8):
            far = levels[np.abs(levels - a[p, g]) >= 10]
            a[p, g + 8] = far[np.random.randint(len(far))]
    return np.exp2(a.ravel()).repeat(32)


BF16 = ml_dtypes.bfloat16


def bf(x):
    return np.asarray(x, np.float32).astype(BF16)


def f64(x):
    return np.asarray(x).astype(np.float64)


N, V, EN1, EN2, D, K, EMB = 1024, 4096, 1024, 512, 128, 512, 1024
BN_EPS = 1e-5


def batchnorm(x):
    m = x.mean(axis=0)
    v = x.var(axis=0)
    return (x - m) * (1.0 / np.sqrt(v + BN_EPS))


def draw0():
    s, t = mx_kscale(EN1), mx_kscale(EN2)
    return {
        "en1": bf(np.maximum(np.random.standard_normal((N, EN1)) * 1.15, 0.0) * s),
        "W2": bf(np.random.standard_normal((EN1, EN2)) / np.sqrt(EN1) / s[:, None] * t),
        "b2": bf(np.random.standard_normal(EN2) * 0.2 * t),
        "Wmean": bf(np.random.standard_normal((EN2, D)) / np.sqrt(EN2) / t[:, None]),
        "Wlogvar": bf(np.random.standard_normal((EN2, D)) / np.sqrt(EN2) / t[:, None]),
        "eps": bf(np.random.standard_normal((N, D))),
    }


def core(en1, W2, b2, Wmean, Wlogvar, eps):
    en2 = np.maximum((mxq(f64(en1), 1, "e4m3") @ mxq(f64(W2), 0, "e4m3")) + f64(b2), 0.0)
    en2q = mxq(en2, 1, "e4m3")
    posterior_mean = batchnorm(en2q @ mxq(f64(Wmean), 0, "e4m3"))
    posterior_logvar = batchnorm(en2q @ mxq(f64(Wlogvar), 0, "e4m3"))
    posterior_var = np.exp(posterior_logvar)
    z = posterior_mean + np.sqrt(posterior_var) * f64(eps)
    zx = batchnorm(z)
    return z, zx


def e4m3fn_bytes(y):
    return np.clip(np.asarray(y, np.float64), -448.0, 448.0).astype(np.float32).astype(ml_dtypes.float8_e4m3fn).view(np.uint8)


def e4m3fn_values(b):
    return np.asarray(b, np.uint8).view(ml_dtypes.float8_e4m3fn).astype(np.float64)


def setup_inputs():
    d = draw0()
    x0 = np.asarray(d['en1']).astype(np.float64)
    s = (np.max(np.abs(x0), axis=(0,), keepdims=True) / 448.0).astype(np.float32)
    out = {}
    for k, v in d.items():
        if k == 'en1':
            out['en1_bytes'] = e4m3fn_bytes(x0 / s.astype(np.float64))
            out['en1_scale'] = s
        else:
            out[k] = v
    return out


def reference(en1_bytes, en1_scale, W2, b2, Wmean, Wlogvar, eps):
    return core(e4m3fn_values(en1_bytes) * en1_scale.astype(np.float64), W2, b2, Wmean, Wlogvar, eps)

@@ -1,0 +1,431 @@
+from contextlib import ExitStack
+
+import concourse.mybir as mybir
+from concourse.masks import make_identity
+
+F32 = mybir.dt.float32
+BF16 = mybir.dt.bfloat16
+U32 = mybir.dt.uint32
+U8 = mybir.dt.uint8
+FP8 = mybir.dt.float8_e4m3fn
+FP8X4 = mybir.dt.float8_e4m3fn_x4
+ADD = mybir.AluOpType.add
+SUB = mybir.AluOpType.subtract
+MULT = mybir.AluOpType.mult
+POW = mybir.AluOpType.pow
+ACT = mybir.ActivationFunctionType
+
+P = 128
+ROWS, K1, K2, D = 1024, 1024, 512, 128
+TILES = ROWS // P
+PASSES = K1 // 512
+CHUNKS = [(0, 2), (2, 2), (4, 2), (6, 1), (7, 1)]
+BN_EPS = 1e-5
+
+FLOPS = 2 * ROWS * K1 * K2 + 2 * ROWS * K2 * D * 2
+
+
+def tile_modelvd_pa_kernel(tc, en1_bytes, en1_scale, w2, b2, w_mean, w_logvar, eps, out_z, out_zx):
+    nc = tc.nc
+    with ExitStack() as ctx:
+        keep = ctx.enter_context(tc.tile_pool(name="keep", bufs=1))
+        ring = ctx.enter_context(tc.tile_pool(name="ring", bufs=3))
+        psum = ctx.enter_context(tc.psum_pool(name="psum", bufs=1))
+        ctx.enter_context(tc.manual_schedule())
+
+        scale_k = keep.tile([P, PASSES, 4], F32, name="scale_k")
+        nc.sync.dma_start(out=scale_k[:], in_=en1_scale.rearrange("o (g p t) -> p (o g) t", p=P, t=4))
+        x_rows = en1_bytes.rearrange("(p i) k -> p i k", i=TILES)
+        x_bytes = []
+        w_raw = []
+        for c in range(4):
+            if c < PASSES:
+                wr = keep.tile([P, 4, K2], BF16, name="wr%d" % c, align_bytes=64)
+                nc.sync.dma_start(out=wr[:], in_=w2[512 * c : 512 * c + 512, :].rearrange("(p j) c -> p j c", j=4))
+                w_raw.append(wr)
+            xb = keep.tile([P, 2, K1], U8, name="xb%d" % c, align_bytes=64)
+            nc.sync.dma_start(out=xb[:], in_=x_rows[:, 2 * c : 2 * c + 2, :])
+            x_bytes.append(xb)
+        b2_raw = keep.tile([P, 4], BF16, name="b2_raw")
+        nc.sync.dma_start(out=b2_raw[:], in_=b2.rearrange("(p t) -> p t", t=4))
+        l_raw = keep.tile([P, 2, 4, D], BF16, name="l_raw", align_bytes=64)
+        nc.sync.dma_start(out=l_raw[:, 0, :, :], in_=w_mean.rearrange("(p j) n -> p j n", j=4))
+        nc.sync.dma_start(out=l_raw[:, 1, :, :], in_=w_logvar.rearrange("(p j) n -> p j n", j=4))
+        eps_raw = keep.tile([P, TILES, D], BF16, name="eps_raw", align_bytes=64)
+        nc.sync.dma_start(out=eps_raw[:], in_=eps.rearrange("(p i) d -> p i d", i=TILES))
+
+        trip = keep.tile([P, 12], F32, name="trip")
+        nc.vector.memset(trip[:], 0.0)
+        nc.vector.memset(trip[:, 0:1], 512.0)
+        nc.vector.memset(trip[:, 5:6], ROWS * BN_EPS)
+        warm = keep.tile([P, 1], F32, name="warm")
+        nc.vector.memset(warm[:], 0.0)
+        warm_out = keep.tile([P, 1], F32, name="warm_out")
+        nc.scalar.activation(out=warm_out[:], in_=warm[:], func=ACT.Exp)
+        ident_f = keep.tile([P, P], F32, name="ident_f")
+        make_identity(nc, ident_f[:])
+        ident_b = keep.tile([P, P], BF16, name="ident_b")
+        make_identity(nc, ident_b[:])
+        neg_half = keep.tile([P, 1], F32, name="neg_half")
+        nc.gpsimd.memset(neg_half[:], -0.5)
+
+        scale_bc = keep.tile([P, K1], F32, name="scale_bc", align_bytes=64)
+        for g in range(PASSES):
+            st = psum.tile([P, 4, P], F32, name="xt%d" % g)
+            for t in range(4):
+                nc.tensor.transpose(st[:, t, :], scale_k[:, g, t : t + 1].to_broadcast([P, P]), ident_f[:])
+            nc.scalar.copy(
+                out=scale_bc[:, 512 * g : 512 * (g + 1)].rearrange("p (m t) -> p m t", t=4),
+                in_=st[:].rearrange("p t m -> p m t"),
+            )
+        b2_col = keep.tile([P, 4], F32, name="b2_col")
+        nc.gpsimd.tensor_copy(out=b2_col[:], in_=b2_raw[:])
+
+        prod = {}
+        turned = {}
+        grouped = {}
+        x_codes = {}
+        x_planes = {}
+        where = {}
+        for c, (first, count) in enumerate(CHUNKS):
+            for ii in range(count):
+                where[first + ii] = (c, ii)
+
+        def product(i):
+            t = ring.tile([P, K1], BF16, name="prod", align_bytes=64)
+            prod[i] = t
+            width = 512 if i == 0 else K1
+            for k in range(0, K1, width):
+                ks = slice(k, k + width)
+                nc.vector.tensor_tensor(
+                    out=t[:, ks], in0=x_bytes[i // 2][:, i % 2, ks].bitcast(FP8), in1=scale_bc[:, ks], op=MULT
+                )
+
+        def turn(i):
+            xt = psum.tile([P, PASSES, 2, P], F32, name="xt%d" % (i % 2))
+            turned[i] = xt
+            words = prod[i][:].bitcast(F32)
+            for g in range(PASSES):
+                for u in range(2):
+                    nc.tensor.transpose(xt[:, g, u, :], words[:, 256 * g + u : 256 * (g + 1) : 2], ident_f[:])
+
+        def empty(i):
+            c, ii = where[i]
+            n = CHUNKS[c][1] * P
+            if ii == 0:
+                gt = ring.tile([P, PASSES, n * 4], BF16, name="gt", align_bytes=64)
+                grouped[c] = gt
+            dst = grouped[c][:].bitcast(F32)[:, :, 256 * ii : 256 * (ii + 1)]
+            nc.scalar.copy(
+                out=dst.rearrange("p g (r u) -> p g r u", u=2), in_=turned[i][:].rearrange("p g u r -> p g r u")
+            )
+
+        def quant_x(c):
+            n = CHUNKS[c][1] * P
+            xc = keep.tile([P, PASSES, n], U32, name="xc%d" % c, align_bytes=64)
+            xs = keep.tile([P, PASSES, n], U8, name="xs%d" % c, align_bytes=64)
+            x_codes[c] = xc
+            x_planes[c] = xs
+            nc.vector.quantize_mx(
+                out=xc[:].rearrange("p g n -> p (g n)").bitcast(FP8X4),
+                scales=xs[:].rearrange("p g n -> p (g n)"),
+                in_=grouped[c][:].rearrange("p g n -> p (g n)"),
+            )
+
+        w_grp = []
+        w_codes = []
+        w_planes = []
+        for g in range(PASSES):
+            w_grp.append(keep.tile([P, 4, P, 4], BF16, name="wg%d" % g, align_bytes=64))
+            w_codes.append(keep.tile([P, K2], U32, name="wc%d" % g, align_bytes=64))
+            w_planes.append(keep.tile([P, K2], U8, name="ws%d" % g, align_bytes=64))
+
+        def weave_w(g, half):
+            src = w_raw[g][:].rearrange("p j (m t) -> p t m j", t=4)
+            ts = slice(2 * half, 2 * half + 2)
+            if (g, half) == (0, 0):
+                nc.vector.tensor_copy(out=w_grp[g][:, ts, :, :], in_=src[:, ts, :, :])
+            else:
+                nc.scalar.copy(out=w_grp[g][:, ts, :, :], in_=src[:, ts, :, :])
+
+        def quant_w(g):
+            nc.vector.quantize_mx(
+                out=w_codes[g][:].bitcast(FP8X4),
+                scales=w_planes[g][:],
+                in_=w_grp[g][:].rearrange("p t m j -> p (t m j)"),
+            )
+
+        l_grp = keep.tile([P, 2, D, 4], BF16, name="l_grp", align_bytes=64)
+        l_codes = keep.tile([P, 2 * D], U32, name="l_codes", align_bytes=64)
+        l_planes = keep.tile([P, 2 * D], U8, name="l_planes", align_bytes=64)
+
+        def weave_l():
+            nc.scalar.copy(out=l_grp[:], in_=l_raw[:].rearrange("p w j n -> p w n j"))
+
+        def quant_l():
+            nc.vector.quantize_mx(
+                out=l_codes[:].bitcast(FP8X4), scales=l_planes[:], in_=l_grp[:].rearrange("p w n j -> p (w n j)")
+            )
+
+        acc = {}
+
+        def mm1(c):
+            n = CHUNKS[c][1] * P
+            for pair in range(2):
+                a = psum.tile([P, 2, n], F32, name="acc%d" % pair)
+                acc[c, pair] = a
+                for tt in range(2):
+                    cols = slice(P * (2 * pair + tt), P * (2 * pair + tt) + P)
+                    for g in range(PASSES):
+                        nc.tensor.matmul_mx(
+                            out=a[:, tt, :],
+                            lhsT=w_codes[g][:, cols].bitcast(FP8X4),
+                            lhsT_scale=w_planes[g][:, cols],
+                            rhs=x_codes[c][:, g, :].bitcast(FP8X4),
+                            rhs_scale=x_planes[c][:, g, :],
+                            start=(g == 0),
+                            stop=(g == PASSES - 1),
+                        )
+
+        hidden = {}
+
+        def relu(c, ts):
+            n = CHUNKS[c][1] * P
+            if c not in hidden:
+                h = ring.tile([P, 4, n], BF16, name="hid", align_bytes=64)
+                hidden[c] = h
+            for t in ts:
+                nc.scalar.activation(
+                    out=hidden[c][:, t, :], in_=acc[c, t // 2][:, t % 2, :], func=ACT.Relu, bias=b2_col[:, t : t + 1]
+                )
+
+        def relu_v(c, ts):
+            for t in ts:
+                nc.vector.tensor_scalar(
+                    out=hidden[c][:, t, :],
+                    in0=acc[c, t // 2][:, t % 2, :],
+                    scalar1=b2_col[:, t : t + 1],
+                    scalar2=0.0,
+                    op0=ADD,
+                    op1=mybir.AluOpType.max,
+                )
+
+        h_grp = {}
+        h_codes = {}
+        h_planes = {}
+
+        def weave_h(c):
+            n = CHUNKS[c][1] * P
+            hg = ring.tile([P, n, 4], BF16, name="hg", align_bytes=64)
+            h_grp[c] = hg
+            dst = hg[:].rearrange("p (c i) t -> p c t i", i=4)
+            src = hidden[c][:].rearrange("p t (c i) -> p c t i", i=4)
+            if c == 0:
+                nc.scalar.copy(out=dst, in_=src)
+            else:
+                nc.vector.tensor_copy(out=dst, in_=src)
+
+        def quant_h(c):
+            n = CHUNKS[c][1] * P
+            hc = ring.tile([P, n], U32, name="hc", align_bytes=64)
+            hs = ring.tile([P, n], U8, name="hs", align_bytes=64)
+            h_codes[c] = hc
+            h_planes[c] = hs
+            nc.vector.quantize_mx(
+                out=hc[:].bitcast(FP8X4), scales=hs[:], in_=h_grp[c][:].rearrange("p n t -> p (n t)")
+            )
+
+        heads = [[psum.tile([P, 512], F32, name="head%d%d" % (w, h)) for h in range(2)] for w in range(2)]
+        stats = [keep.tile([P, 3, 6], F32, name="stats%d" % w) for w in range(2)]
+
+        def place(c):
+            first, count = CHUNKS[c]
+            return first // 4, slice((first % 4) * P, (first % 4 + count) * P)
+
+        def mm2(c):
+            h, cols = place(c)
+            for w in (1, 0):
+                nc.tensor.matmul_mx(
+                    out=heads[w][h][:, cols],
+                    lhsT=l_codes[:, D * w : D * w + D].bitcast(FP8X4),
+                    lhsT_scale=l_planes[:, D * w : D * w + D],
+                    rhs=h_codes[c][:].bitcast(FP8X4),
+                    rhs_scale=h_planes[c][:],
+                    start=True,
+                    stop=True,
+                )
+
+        def stat(part, ws=(1, 0)):
+            h, cols = ((0, slice(0, 512)), (1, slice(0, 384)), (1, slice(384, 512)))[part]
+            for w in ws:
+                nc.vector.bn_stats(out=stats[w][:, part, :], in_=heads[w][h][:, cols])
+
+        eps_t = keep.tile([P, ROWS], BF16, name="eps_t", align_bytes=64)
+
+        def turn_eps():
+            et = psum.tile([P, TILES, P], BF16, name="xt0")
+            for i in range(TILES):
+                nc.tensor.transpose(et[:, i, :], eps_raw[:, i, :], ident_b[:])
+            nc.scalar.copy(out=eps_t[:], in_=et[:].rearrange("p i r -> p (i r)"))
+
+        weave_w(0, 0)
+        product(0)
+        weave_w(0, 1)
+        turn(0)
+        product(1)
+        empty(0)
+        turn(1)
+        weave_w(1, 0)
+        product(2)
+        empty(1)
+        turn(2)
+        weave_w(1, 1)
+        product(3)
+        empty(2)
+        turn(3)
+        quant_x(0)
+        empty(3)
+        quant_w(0)
+        quant_w(1)
+        mm1(0)
+        product(4)
+        weave_l()
+        turn(4)
+        relu(0, (0, 1, 2, 3))
+        quant_x(1)
+        empty(4)
+        product(5)
+        mm1(1)
+        turn(5)
+        weave_h(0)
+        quant_l()
+        product(6)
+        empty(5)
+        turn(6)
+        quant_h(0)
+        mm2(0)
+        relu(1, (0, 1, 2, 3))
+        product(7)
+        quant_x(2)
+        empty(6)
+        turn(7)
+        mm1(2)
+        empty(7)
+        weave_h(1)
+        quant_x(3)
+        quant_h(1)
+        mm2(1)
+        relu(2, (0, 1, 2, 3))
+        mm1(3)
+        quant_x(4)
+        turn_eps()
+        stat(0)
+        relu(3, (0, 1))
+        weave_h(2)
+        relu_v(3, (2, 3))
+        quant_h(2)
+        mm1(4)
+        mm2(2)
+        weave_h(3)
+        relu(4, (0, 1))
+        relu_v(4, (2, 3))
+        quant_h(3)
+        mm2(3)
+        weave_h(4)
+        quant_h(4)
+        mm2(4)
+        stat(1)
+
+        mv = [keep.tile([P, 2], F32, name="mv%d" % w) for w in range(2)]
+        nmu = [keep.tile([P, 1], F32, name="nmu%d" % w) for w in range(2)]
+        ve = [keep.tile([P, 1], F32, name="ve%d" % w) for w in range(2)]
+        rs = [keep.tile([P, 1], F32, name="rs%d" % w) for w in range(2)]
+        nb = [keep.tile([P, 1], F32, name="nb%d" % w) for w in range(2)]
+        for w, gain in ((1, 4.0), (0, 1.0)):
+            stat(2, (w,))
+            nc.vector.bn_aggr(out=mv[w][:], in_=stats[w][:].rearrange("p c s -> p (c s)"))
+            nc.vector.tensor_scalar(
+                out=ve[w][:], in0=mv[w][:, 1:2], scalar1=gain, scalar2=gain * BN_EPS, op0=MULT, op1=ADD
+            )
+            nc.gpsimd.tensor_scalar(out=nmu[w][:], in0=mv[w][:, 0:1], scalar1=-1.0, scalar2=None, op0=MULT)
+            nc.gpsimd.tensor_tensor(out=rs[w][:], in0=ve[w][:], in1=neg_half[:], op=POW)
+            nc.gpsimd.tensor_tensor(out=nb[w][:], in0=nmu[w][:], in1=rs[w][:], op=MULT)
+        dev = keep.tile([P, 2, 512], F32, name="dev", align_bytes=64)
+        noise = keep.tile([P, 2, 512], F32, name="noise", align_bytes=64)
+        z_t = keep.tile([P, 2, 512], F32, name="z_t", align_bytes=64)
+        zf_t = keep.tile([P, 2, 512], F32, name="zf_t", align_bytes=64)
+        zx_t = keep.tile([P, 2, 512], F32, name="zx_t", align_bytes=64)
+        junk = keep.tile([P, 512], F32, name="junk", align_bytes=64)
+        sums = keep.tile([P, 2], F32, name="sums")
+        nmean = keep.tile([P, 1], F32, name="nmean")
+
+        z_bank = {}
+
+        def turn_back(src, h, name):
+            b = psum.tile([P, 4, P], F32, name=name)
+            for i in range(4):
+                nc.tensor.transpose(b[:, i, :], src[:, h, P * i : P * i + P], ident_f[:])
+            return b
+
+        def noise_of(h):
+            nc.vector.tensor_tensor(
+                out=noise[:, h, :], in0=dev[:, h, :], in1=eps_t[:, 512 * h : 512 * h + 512], op=MULT
+            )
+
+        def sample(h):
+            nc.vector.scalar_tensor_tensor(
+                out=z_t[:, h, :], in0=heads[0][h][:], scalar=rs[0][:], in1=noise[:, h, :], op0=MULT, op1=ADD
+            )
+
+        for h in range(2):
+            nc.scalar.activation(out=dev[:, h, :], in_=heads[1][h][:], func=ACT.Exp, bias=nb[1][:], scale=rs[1][:])
+        noise_of(0)
+        sample(0)
+        nc.scalar.activation(
+            out=zf_t[:, 0, :], in_=z_t[:, 0, :], func=ACT.Identity, bias=nb[0][:], accum_out=sums[:, 0:1]
+        )
+        noise_of(1)
+        nc.scalar.activation(out=junk[:], in_=zf_t[:, 0, :], func=ACT.Square, accum_out=sums[:, 1:2])
+        z_bank[0] = turn_back(zf_t, 0, "xt0")
+        sample(1)
+        nc.scalar.activation(out=zf_t[:, 1, :], in_=z_t[:, 1, :], func=ACT.Identity, bias=nb[0][:])
+        z_bank[1] = turn_back(zf_t, 1, "xt1")
+        nc.vector.tensor_scalar(
+            out=trip[:, 1:2], in0=sums[:, 0:1], scalar1=1.0 / 512, scalar2=nb[0][:], op0=MULT, op1=SUB
+        )
+        nc.vector.tensor_scalar(out=nmean[:], in0=sums[:, 0:1], scalar1=-1.0 / 512, scalar2=None, op0=MULT)
+        nc.vector.bn_stats(out=trip[:, 6:12], in_=z_t[:, 1, :])
+        nc.vector.scalar_tensor_tensor(
+            out=trip[:, 2:3], in0=sums[:, 0:1], scalar=nmean[:], in1=sums[:, 1:2], op0=MULT, op1=ADD
+        )
+        mvz = keep.tile([P, 2], F32, name="mvz")
+        rsz = keep.tile([P, 1], F32, name="rsz")
+        nc.vector.bn_aggr(out=mvz[:], in_=trip[:])
+        nc.gpsimd.tensor_tensor(out=rsz[:], in0=mvz[:, 1:2], in1=neg_half[:], op=POW)
+
+        z_out = keep.tile([P, TILES, P], F32, name="z_out", align_bytes=64)
+        zx_out = keep.tile([P, TILES, P], F32, name="zx_out", align_bytes=64)
+        z_rows = out_z.rearrange("(p i) d -> p i d", i=TILES)
+        zx_bank = []
+        zx_rows = out_zx.rearrange("(p i) d -> p i d", i=TILES)
+        for h in range(2):
+            cols = slice(4 * h, 4 * h + 4)
+            nc.scalar.copy(out=z_out[:, cols, :], in_=z_bank[h][:])
+            nc.sync.dma_start(out=z_rows[:, cols, :], in_=z_out[:, cols, :])
+        for q in range(4):
+            cols = slice(2 * q, 2 * q + 2)
+            part = slice(256 * (q % 2), 256 * (q % 2) + 256)
+            nc.vector.tensor_scalar(
+                out=zx_t[:, q // 2, part], in0=z_t[:, q // 2, part], scalar1=mvz[:, 0:1], scalar2=rsz[:], op0=SUB, op1=MULT
+            )
+            b = psum.tile([P, 2, P], F32, name=("acc0", "acc1", "head00", "head01")[q])
+            for i in range(2):
+                nc.tensor.transpose(b[:, i, :], zx_t[:, q // 2, 256 * (q % 2) + P * i : 256 * (q % 2) + P * i + P], ident_f[:])
+            zx_bank.append(b)
+        for q in range(4):
+            cols = slice(2 * q, 2 * q + 2)
+            if q % 2 == 0:
+                nc.scalar.copy(out=zx_out[:, cols, :], in_=zx_bank[q][:])
+            else:
+                nc.vector.tensor_copy(out=zx_out[:, cols, :], in_=zx_bank[q][:])
+            nc.sync.dma_start(out=zx_rows[:, cols, :], in_=zx_out[:, cols, :])

@@ -20,6 +20,7 @@ ROWS, K1, K2, D = 1024, 1024, 512, 128
 TILES = ROWS // P
 PASSES = K1 // 512
 CHUNKS = [(0, 2), (2, 2), (4, 2), (6, 1), (7, 1)]
+ADDED = (3, 4)
 BN_EPS = 1e-5
 
 FLOPS = 2 * ROWS * K1 * K2 + 2 * ROWS * K2 * D * 2
@@ -29,7 +30,7 @@ def tile_modelvd_pa_kernel(tc, en1_bytes, en1_scale, w2, b2, w_mean, w_logvar, e
     nc = tc.nc
     with ExitStack() as ctx:
         keep = ctx.enter_context(tc.tile_pool(name="keep", bufs=1))
-        ring = ctx.enter_context(tc.tile_pool(name="ring", bufs=3))
+        ring = ctx.enter_context(tc.tile_pool(name="ring", bufs=6))
         psum = ctx.enter_context(tc.psum_pool(name="psum", bufs=1))
         ctx.enter_context(tc.manual_schedule())
 
@@ -39,13 +40,13 @@ def tile_modelvd_pa_kernel(tc, en1_bytes, en1_scale, w2, b2, w_mean, w_logvar, e
         x_bytes = []
         w_raw = []
         for c in range(4):
+            xb = keep.tile([P, 2, K1], U8, name="xb%d" % c, align_bytes=64)
+            nc.sync.dma_start(out=xb[:], in_=x_rows[:, 2 * c : 2 * c + 2, :])
+            x_bytes.append(xb)
             if c < PASSES:
                 wr = keep.tile([P, 4, K2], BF16, name="wr%d" % c, align_bytes=64)
                 nc.sync.dma_start(out=wr[:], in_=w2[512 * c : 512 * c + 512, :].rearrange("(p j) c -> p j c", j=4))
                 w_raw.append(wr)
-            xb = keep.tile([P, 2, K1], U8, name="xb%d" % c, align_bytes=64)
-            nc.sync.dma_start(out=xb[:], in_=x_rows[:, 2 * c : 2 * c + 2, :])
-            x_bytes.append(xb)
         b2_raw = keep.tile([P, 4], BF16, name="b2_raw")
         nc.sync.dma_start(out=b2_raw[:], in_=b2.rearrange("(p t) -> p t", t=4))
         l_raw = keep.tile([P, 2, 4, D], BF16, name="l_raw", align_bytes=64)
@@ -58,6 +59,10 @@ def tile_modelvd_pa_kernel(tc, en1_bytes, en1_scale, w2, b2, w_mean, w_logvar, e
         nc.vector.memset(trip[:], 0.0)
         nc.vector.memset(trip[:, 0:1], 512.0)
         nc.vector.memset(trip[:, 5:6], ROWS * BN_EPS)
+        stats = [keep.tile([P, 21], F32, name="stats%d" % w) for w in range(2)]
+        for w in range(2):
+            nc.vector.memset(stats[w][:, 18:20], 0.0)
+            nc.vector.memset(stats[w][:, 20:21], ROWS * BN_EPS)
         warm = keep.tile([P, 1], F32, name="warm")
         nc.vector.memset(warm[:], 0.0)
         warm_out = keep.tile([P, 1], F32, name="warm_out")
@@ -74,7 +79,8 @@ def tile_modelvd_pa_kernel(tc, en1_bytes, en1_scale, w2, b2, w_mean, w_logvar, e
             st = psum.tile([P, 4, P], F32, name="xt%d" % g)
             for t in range(4):
                 nc.tensor.transpose(st[:, t, :], scale_k[:, g, t : t + 1].to_broadcast([P, P]), ident_f[:])
-            nc.scalar.copy(
+            copy = (nc.vector.tensor_copy, nc.scalar.copy)[g]
+            copy(
                 out=scale_bc[:, 512 * g : 512 * (g + 1)].rearrange("p (m t) -> p m t", t=4),
                 in_=st[:].rearrange("p t m -> p m t"),
             )
@@ -102,7 +108,7 @@ def tile_modelvd_pa_kernel(tc, en1_bytes, en1_scale, w2, b2, w_mean, w_logvar, e
                 )
 
         def turn(i):
-            xt = psum.tile([P, PASSES, 2, P], F32, name="xt%d" % (i % 2))
+            xt = psum.tile([P, PASSES, 2, P], F32, name=("xt0", "xt1", "head01", "head11")[i % 4])
             turned[i] = xt
             words = prod[i][:].bitcast(F32)
             for g in range(PASSES):
@@ -143,10 +149,7 @@ def tile_modelvd_pa_kernel(tc, en1_bytes, en1_scale, w2, b2, w_mean, w_logvar, e
         def weave_w(g, half):
             src = w_raw[g][:].rearrange("p j (m t) -> p t m j", t=4)
             ts = slice(2 * half, 2 * half + 2)
-            if (g, half) == (0, 0):
-                nc.vector.tensor_copy(out=w_grp[g][:, ts, :, :], in_=src[:, ts, :, :])
-            else:
-                nc.scalar.copy(out=w_grp[g][:, ts, :, :], in_=src[:, ts, :, :])
+            nc.scalar.copy(out=w_grp[g][:, ts, :, :], in_=src[:, ts, :, :])
 
         def quant_w(g):
             nc.vector.quantize_mx(
@@ -169,12 +172,15 @@ def tile_modelvd_pa_kernel(tc, en1_bytes, en1_scale, w2, b2, w_mean, w_logvar, e
 
         acc = {}
 
-        def mm1(c):
+        def mm1(c, pair):
             n = CHUNKS[c][1] * P
-            for pair in range(2):
+            if c in ADDED:
+                a = psum.tile([P, 4, n], F32, name="acc%d" % ((c + 1) % 2))
+            else:
                 a = psum.tile([P, 2, n], F32, name="acc%d" % pair)
+            if True:
                 acc[c, pair] = a
-                for tt in range(2):
+                for tt in range(4 if c in ADDED else 2):
                     cols = slice(P * (2 * pair + tt), P * (2 * pair + tt) + P)
                     for g in range(PASSES):
                         nc.tensor.matmul_mx(
@@ -188,6 +194,7 @@ def tile_modelvd_pa_kernel(tc, en1_bytes, en1_scale, w2, b2, w_mean, w_logvar, e
                         )
 
         hidden = {}
+        h_grp = {}
 
         def relu(c, ts):
             n = CHUNKS[c][1] * P
@@ -198,6 +205,19 @@ def tile_modelvd_pa_kernel(tc, en1_bytes, en1_scale, w2, b2, w_mean, w_logvar, e
                 nc.scalar.activation(
                     out=hidden[c][:, t, :], in_=acc[c, t // 2][:, t % 2, :], func=ACT.Relu, bias=b2_col[:, t : t + 1]
                 )
+
+        def add_b2(c):
+            hg = ring.tile([P, P, 4], BF16, name="hg", align_bytes=64)
+            h_grp[c] = hg
+            nc.vector.tensor_tensor(
+                out=hg[:],
+                in0=acc[c, 0][:].rearrange("p t n -> p n t"),
+                in1=b2_col[:].unsqueeze(1).to_broadcast([P, P, 4]),
+                op=ADD,
+            )
+
+        def relu_in_place(c):
+            nc.scalar.activation(out=h_grp[c][:], in_=h_grp[c][:], func=ACT.Relu)
 
         def relu_v(c, ts):
             for t in ts:
@@ -210,7 +230,6 @@ def tile_modelvd_pa_kernel(tc, en1_bytes, en1_scale, w2, b2, w_mean, w_logvar, e
                     op1=mybir.AluOpType.max,
                 )
 
-        h_grp = {}
         h_codes = {}
         h_planes = {}
 
@@ -220,7 +239,7 @@ def tile_modelvd_pa_kernel(tc, en1_bytes, en1_scale, w2, b2, w_mean, w_logvar, e
             h_grp[c] = hg
             dst = hg[:].rearrange("p (c i) t -> p c t i", i=4)
             src = hidden[c][:].rearrange("p t (c i) -> p c t i", i=4)
-            if c == 0:
+            if c == 2:
                 nc.scalar.copy(out=dst, in_=src)
             else:
                 nc.vector.tensor_copy(out=dst, in_=src)
@@ -235,8 +254,7 @@ def tile_modelvd_pa_kernel(tc, en1_bytes, en1_scale, w2, b2, w_mean, w_logvar, e
                 out=hc[:].bitcast(FP8X4), scales=hs[:], in_=h_grp[c][:].rearrange("p n t -> p (n t)")
             )
 
-        heads = [[psum.tile([P, 512], F32, name="head%d%d" % (w, h)) for h in range(2)] for w in range(2)]
-        stats = [keep.tile([P, 3, 6], F32, name="stats%d" % w) for w in range(2)]
+        heads = [{}, {}]
 
         def place(c):
             first, count = CHUNKS[c]
@@ -245,6 +263,9 @@ def tile_modelvd_pa_kernel(tc, en1_bytes, en1_scale, w2, b2, w_mean, w_logvar, e
         def mm2(c):
             h, cols = place(c)
             for w in (1, 0):
+                if h not in heads[w]:
+                    head = psum.tile([P, 512], F32, name="head%d%d" % (w, h))
+                    heads[w][h] = head
                 nc.tensor.matmul_mx(
                     out=heads[w][h][:, cols],
                     lhsT=l_codes[:, D * w : D * w + D].bitcast(FP8X4),
@@ -258,98 +279,113 @@ def tile_modelvd_pa_kernel(tc, en1_bytes, en1_scale, w2, b2, w_mean, w_logvar, e
         def stat(part, ws=(1, 0)):
             h, cols = ((0, slice(0, 512)), (1, slice(0, 384)), (1, slice(384, 512)))[part]
             for w in ws:
-                nc.vector.bn_stats(out=stats[w][:, part, :], in_=heads[w][h][:, cols])
+                nc.vector.bn_stats(out=stats[w][:, 6 * part : 6 * part + 6], in_=heads[w][h][:, cols])
 
+        eps_bank = []
         eps_t = keep.tile([P, ROWS], BF16, name="eps_t", align_bytes=64)
 
         def turn_eps():
             et = psum.tile([P, TILES, P], BF16, name="xt0")
             for i in range(TILES):
                 nc.tensor.transpose(et[:, i, :], eps_raw[:, i, :], ident_b[:])
-            nc.scalar.copy(out=eps_t[:], in_=et[:].rearrange("p i r -> p (i r)"))
+            eps_bank.append(et)
 
-        weave_w(0, 0)
+        def empty_eps():
+            nc.scalar.copy(out=eps_t[:], in_=eps_bank[0][:].rearrange("p i r -> p (i r)"))
+
         product(0)
-        weave_w(0, 1)
-        turn(0)
+        weave_w(0, 0)
         product(1)
-        empty(0)
-        turn(1)
-        weave_w(1, 0)
+        turn(0)
+        weave_w(0, 1)
         product(2)
-        empty(1)
-        turn(2)
-        weave_w(1, 1)
-        product(3)
-        empty(2)
-        turn(3)
-        quant_x(0)
-        empty(3)
+        turn(1)
+        empty(0)
+        weave_w(1, 0)
         quant_w(0)
-        quant_w(1)
-        mm1(0)
+        turn(2)
+        product(3)
+        empty(1)
+        weave_w(1, 1)
+        quant_x(0)
+        turn(3)
         product(4)
+        empty(2)
         weave_l()
+        quant_w(1)
         turn(4)
-        relu(0, (0, 1, 2, 3))
-        quant_x(1)
-        empty(4)
         product(5)
-        mm1(1)
-        turn(5)
-        weave_h(0)
+        mm1(0, 0)
+        empty(3)
+        empty(4)
         quant_l()
+        turn(5)
         product(6)
+        relu(0, (0, 1))
+        mm1(0, 1)
         empty(5)
+        quant_x(1)
         turn(6)
-        quant_h(0)
-        mm2(0)
-        relu(1, (0, 1, 2, 3))
+        relu(0, (2, 3))
         product(7)
-        quant_x(2)
+        mm1(1, 0)
         empty(6)
+        mm1(1, 1)
+        quant_x(2)
+        relu(1, (0, 1))
         turn(7)
-        mm1(2)
+        weave_h(0)
+        relu(1, (2,))
+        mm1(2, 0)
         empty(7)
-        weave_h(1)
+        relu_v(1, (3,))
+        quant_h(0)
+        relu(2, (0, 1))
+        mm1(2, 1)
         quant_x(3)
-        quant_h(1)
-        mm2(1)
-        relu(2, (0, 1, 2, 3))
-        mm1(3)
+        weave_h(1)
+        mm2(0)
+        relu(2, (2, 3))
+        mm1(3, 0)
         quant_x(4)
-        turn_eps()
-        stat(0)
-        relu(3, (0, 1))
+        quant_h(1)
+        mm1(4, 0)
         weave_h(2)
-        relu_v(3, (2, 3))
+        add_b2(3)
+        turn_eps()
+        add_b2(4)
+        mm2(1)
+        relu_in_place(3)
+        relu_in_place(4)
         quant_h(2)
-        mm1(4)
-        mm2(2)
-        weave_h(3)
-        relu(4, (0, 1))
-        relu_v(4, (2, 3))
         quant_h(3)
+        stat(0, (1,))
+        empty_eps()
         mm2(3)
-        weave_h(4)
+        mm2(2)
         quant_h(4)
+        stat(0, (0,))
         mm2(4)
-        stat(1)
+        stat(1, (1,))
 
         mv = [keep.tile([P, 2], F32, name="mv%d" % w) for w in range(2)]
-        nmu = [keep.tile([P, 1], F32, name="nmu%d" % w) for w in range(2)]
-        ve = [keep.tile([P, 1], F32, name="ve%d" % w) for w in range(2)]
         rs = [keep.tile([P, 1], F32, name="rs%d" % w) for w in range(2)]
         nb = [keep.tile([P, 1], F32, name="nb%d" % w) for w in range(2)]
-        for w, gain in ((1, 4.0), (0, 1.0)):
-            stat(2, (w,))
-            nc.vector.bn_aggr(out=mv[w][:], in_=stats[w][:].rearrange("p c s -> p (c s)"))
-            nc.vector.tensor_scalar(
-                out=ve[w][:], in0=mv[w][:, 1:2], scalar1=gain, scalar2=gain * BN_EPS, op0=MULT, op1=ADD
-            )
-            nc.gpsimd.tensor_scalar(out=nmu[w][:], in0=mv[w][:, 0:1], scalar1=-1.0, scalar2=None, op0=MULT)
-            nc.gpsimd.tensor_tensor(out=rs[w][:], in0=ve[w][:], in1=neg_half[:], op=POW)
-            nc.gpsimd.tensor_tensor(out=nb[w][:], in0=nmu[w][:], in1=rs[w][:], op=MULT)
+        half_rs = keep.tile([P, 1], F32, name="half_rs")
+        stat(2, (1,))
+        nc.vector.bn_aggr(out=mv[1][:], in_=stats[1][:])
+        nc.gpsimd.tensor_tensor(out=rs[1][:], in0=mv[1][:, 1:2], in1=neg_half[:], op=POW)
+        stat(1, (0,))
+        nc.vector.scalar_tensor_tensor(
+            out=nb[1][:], in0=mv[1][:, 0:1], scalar=-0.5, in1=rs[1][:], op0=MULT, op1=MULT
+        )
+        nc.vector.tensor_scalar(out=half_rs[:], in0=rs[1][:], scalar1=0.5, scalar2=None, op0=MULT)
+        stat(2, (0,))
+        nc.vector.bn_aggr(out=mv[0][:], in_=stats[0][:])
+        nc.gpsimd.tensor_tensor(out=rs[0][:], in0=mv[0][:, 1:2], in1=neg_half[:], op=POW)
+        nc.vector.scalar_tensor_tensor(
+            out=nb[0][:], in0=mv[0][:, 0:1], scalar=-1.0, in1=rs[0][:], op0=MULT, op1=MULT
+        )
         dev = keep.tile([P, 2, 512], F32, name="dev", align_bytes=64)
         noise = keep.tile([P, 2, 512], F32, name="noise", align_bytes=64)
         z_t = keep.tile([P, 2, 512], F32, name="z_t", align_bytes=64)
@@ -367,9 +403,12 @@ def tile_modelvd_pa_kernel(tc, en1_bytes, en1_scale, w2, b2, w_mean, w_logvar, e
                 nc.tensor.transpose(b[:, i, :], src[:, h, P * i : P * i + P], ident_f[:])
             return b
 
-        def noise_of(h):
+        def noise_of(h, part=slice(0, 512)):
             nc.vector.tensor_tensor(
-                out=noise[:, h, :], in0=dev[:, h, :], in1=eps_t[:, 512 * h : 512 * h + 512], op=MULT
+                out=noise[:, h, part],
+                in0=dev[:, h, part],
+                in1=eps_t[:, 512 * h + part.start : 512 * h + part.stop],
+                op=MULT,
             )
 
         def sample(h):
@@ -377,9 +416,12 @@ def tile_modelvd_pa_kernel(tc, en1_bytes, en1_scale, w2, b2, w_mean, w_logvar, e
                 out=z_t[:, h, :], in0=heads[0][h][:], scalar=rs[0][:], in1=noise[:, h, :], op0=MULT, op1=ADD
             )
 
-        for h in range(2):
-            nc.scalar.activation(out=dev[:, h, :], in_=heads[1][h][:], func=ACT.Exp, bias=nb[1][:], scale=rs[1][:])
-        noise_of(0)
+        for h, part in ((0, slice(0, 256)), (0, slice(256, 512)), (1, slice(0, 512))):
+            nc.scalar.activation(
+                out=dev[:, h, part], in_=heads[1][h][:, part], func=ACT.Exp, bias=nb[1][:], scale=half_rs[:]
+            )
+        noise_of(0, slice(0, 256))
+        noise_of(0, slice(256, 512))
         sample(0)
         nc.scalar.activation(
             out=zf_t[:, 0, :], in_=z_t[:, 0, :], func=ACT.Identity, bias=nb[0][:], accum_out=sums[:, 0:1]
@@ -418,7 +460,7 @@ def tile_modelvd_pa_kernel(tc, en1_bytes, en1_scale, w2, b2, w_mean, w_logvar, e
             nc.vector.tensor_scalar(
                 out=zx_t[:, q // 2, part], in0=z_t[:, q // 2, part], scalar1=mvz[:, 0:1], scalar2=rsz[:], op0=SUB, op1=MULT
             )
-            b = psum.tile([P, 2, P], F32, name=("acc0", "acc1", "head00", "head01")[q])
+            b = psum.tile([P, 2, P], F32, name=("acc0", "acc1", "head10", "head11")[q])
             for i in range(2):
                 nc.tensor.transpose(b[:, i, :], zx_t[:, q // 2, 256 * (q % 2) + P * i : 256 * (q % 2) + P * i + P], ident_f[:])
             zx_bank.append(b)

@@ -40,13 +40,13 @@ def tile_modelvd_pa_kernel(tc, en1_bytes, en1_scale, w2, b2, w_mean, w_logvar, e
         x_bytes = []
         w_raw = []
         for c in range(4):
-            xb = keep.tile([P, 2, K1], U8, name="xb%d" % c, align_bytes=64)
-            nc.sync.dma_start(out=xb[:], in_=x_rows[:, 2 * c : 2 * c + 2, :])
-            x_bytes.append(xb)
             if c < PASSES:
                 wr = keep.tile([P, 4, K2], BF16, name="wr%d" % c, align_bytes=64)
                 nc.sync.dma_start(out=wr[:], in_=w2[512 * c : 512 * c + 512, :].rearrange("(p j) c -> p j c", j=4))
                 w_raw.append(wr)
+            xb = keep.tile([P, 2, K1], U8, name="xb%d" % c, align_bytes=64)
+            nc.sync.dma_start(out=xb[:], in_=x_rows[:, 2 * c : 2 * c + 2, :])
+            x_bytes.append(xb)
         b2_raw = keep.tile([P, 4], BF16, name="b2_raw")
         nc.sync.dma_start(out=b2_raw[:], in_=b2.rearrange("(p t) -> p t", t=4))
         l_raw = keep.tile([P, 2, 4, D], BF16, name="l_raw", align_bytes=64)
@@ -55,7 +55,7 @@ def tile_modelvd_pa_kernel(tc, en1_bytes, en1_scale, w2, b2, w_mean, w_logvar, e
         eps_raw = keep.tile([P, TILES, D], BF16, name="eps_raw", align_bytes=64)
         nc.sync.dma_start(out=eps_raw[:], in_=eps.rearrange("(p i) d -> p i d", i=TILES))
 
-        trip = keep.tile([P, 12], F32, name="trip")
+        trip = keep.tile([P, 18], F32, name="trip")
         nc.vector.memset(trip[:], 0.0)
         nc.vector.memset(trip[:, 0:1], 512.0)
         nc.vector.memset(trip[:, 5:6], ROWS * BN_EPS)
@@ -85,7 +85,6 @@ def tile_modelvd_pa_kernel(tc, en1_bytes, en1_scale, w2, b2, w_mean, w_logvar, e
                 in_=st[:].rearrange("p t m -> p m t"),
             )
         b2_col = keep.tile([P, 4], F32, name="b2_col")
-        nc.gpsimd.tensor_copy(out=b2_col[:], in_=b2_raw[:])
 
         prod = {}
         turned = {}
@@ -149,7 +148,12 @@ def tile_modelvd_pa_kernel(tc, en1_bytes, en1_scale, w2, b2, w_mean, w_logvar, e
         def weave_w(g, half):
             src = w_raw[g][:].rearrange("p j (m t) -> p t m j", t=4)
             ts = slice(2 * half, 2 * half + 2)
-            nc.scalar.copy(out=w_grp[g][:, ts, :, :], in_=src[:, ts, :, :])
+            if (g, half) == (0, 0):
+                nc.gpsimd.tensor_scalar(
+                    out=w_grp[g][:, ts, :, :], in0=src[:, ts, :, :], scalar1=1.0, scalar2=0.0, op0=MULT, op1=ADD
+                )
+            else:
+                nc.scalar.copy(out=w_grp[g][:, ts, :, :], in_=src[:, ts, :, :])
 
         def quant_w(g):
             nc.vector.quantize_mx(
@@ -220,6 +224,10 @@ def tile_modelvd_pa_kernel(tc, en1_bytes, en1_scale, w2, b2, w_mean, w_logvar, e
             nc.scalar.activation(out=h_grp[c][:], in_=h_grp[c][:], func=ACT.Relu)
 
         def relu_v(c, ts):
+            n = CHUNKS[c][1] * P
+            if c not in hidden:
+                h = ring.tile([P, 4, n], BF16, name="hid", align_bytes=64)
+                hidden[c] = h
             for t in ts:
                 nc.vector.tensor_scalar(
                     out=hidden[c][:, t, :],
@@ -239,7 +247,7 @@ def tile_modelvd_pa_kernel(tc, en1_bytes, en1_scale, w2, b2, w_mean, w_logvar, e
             h_grp[c] = hg
             dst = hg[:].rearrange("p (c i) t -> p c t i", i=4)
             src = hidden[c][:].rearrange("p t (c i) -> p c t i", i=4)
-            if c == 2:
+            if c != 1:
                 nc.scalar.copy(out=dst, in_=src)
             else:
                 nc.vector.tensor_copy(out=dst, in_=src)
@@ -293,78 +301,80 @@ def tile_modelvd_pa_kernel(tc, en1_bytes, en1_scale, w2, b2, w_mean, w_logvar, e
         def empty_eps():
             nc.scalar.copy(out=eps_t[:], in_=eps_bank[0][:].rearrange("p i r -> p (i r)"))
 
-        product(0)
         weave_w(0, 0)
-        product(1)
-        turn(0)
+        nc.gpsimd.tensor_copy(out=b2_col[:], in_=b2_raw[:])
+        product(0)
         weave_w(0, 1)
+        turn(0)
+        product(1)
+        weave_w(1, 0)
         product(2)
         turn(1)
         empty(0)
-        weave_w(1, 0)
+        weave_w(1, 1)
         quant_w(0)
         turn(2)
         product(3)
         empty(1)
-        weave_w(1, 1)
-        quant_x(0)
-        turn(3)
-        product(4)
-        empty(2)
-        weave_l()
         quant_w(1)
-        turn(4)
-        product(5)
+        empty(2)
+        turn(3)
+        weave_l()
+        quant_x(0)
+        product(4)
         mm1(0, 0)
         empty(3)
+        mm1(0, 1)
+        product(5)
+        relu(0, (0, 1))
+        turn(4)
+        relu(0, (3,))
+        quant_x(1)
         empty(4)
-        quant_l()
         turn(5)
         product(6)
-        relu(0, (0, 1))
-        mm1(0, 1)
-        empty(5)
-        quant_x(1)
-        turn(6)
-        relu(0, (2, 3))
-        product(7)
+        relu(0, (2,))
         mm1(1, 0)
-        empty(6)
-        mm1(1, 1)
-        quant_x(2)
-        relu(1, (0, 1))
-        turn(7)
+        empty(5)
         weave_h(0)
-        relu(1, (2,))
+        mm1(1, 1)
+        quant_l()
+        quant_x(2)
+        turn(6)
+        relu_v(1, (0,))
+        turn_eps()
+        relu(1, (1,))
+        product(7)
+        empty(6)
         mm1(2, 0)
-        empty(7)
-        relu_v(1, (3,))
+        relu(1, (2, 3))
+        quant_x(3)
+        turn(7)
         quant_h(0)
         relu(2, (0, 1))
-        mm1(2, 1)
-        quant_x(3)
         weave_h(1)
-        mm2(0)
-        relu(2, (2, 3))
+        mm1(2, 1)
+        empty(7)
         mm1(3, 0)
-        quant_x(4)
         quant_h(1)
+        relu(2, (2, 3))
+        quant_x(4)
+        mm2(0)
+        mm2(1)
+        add_b2(3)
         mm1(4, 0)
         weave_h(2)
-        add_b2(3)
-        turn_eps()
-        add_b2(4)
-        mm2(1)
-        relu_in_place(3)
-        relu_in_place(4)
-        quant_h(2)
-        quant_h(3)
         stat(0, (1,))
+        add_b2(4)
+        relu_in_place(3)
+        quant_h(2)
+        relu_in_place(4)
+        mm2(2)
+        quant_h(3)
+        stat(0, (0,))
         empty_eps()
         mm2(3)
-        mm2(2)
         quant_h(4)
-        stat(0, (0,))
         mm2(4)
         stat(1, (1,))
 
@@ -383,9 +393,6 @@ def tile_modelvd_pa_kernel(tc, en1_bytes, en1_scale, w2, b2, w_mean, w_logvar, e
         stat(2, (0,))
         nc.vector.bn_aggr(out=mv[0][:], in_=stats[0][:])
         nc.gpsimd.tensor_tensor(out=rs[0][:], in0=mv[0][:, 1:2], in1=neg_half[:], op=POW)
-        nc.vector.scalar_tensor_tensor(
-            out=nb[0][:], in0=mv[0][:, 0:1], scalar=-1.0, in1=rs[0][:], op0=MULT, op1=MULT
-        )
         dev = keep.tile([P, 2, 512], F32, name="dev", align_bytes=64)
         noise = keep.tile([P, 2, 512], F32, name="noise", align_bytes=64)
         z_t = keep.tile([P, 2, 512], F32, name="z_t", align_bytes=64)
@@ -403,40 +410,50 @@ def tile_modelvd_pa_kernel(tc, en1_bytes, en1_scale, w2, b2, w_mean, w_logvar, e
                 nc.tensor.transpose(b[:, i, :], src[:, h, P * i : P * i + P], ident_f[:])
             return b
 
-        def noise_of(h, part=slice(0, 512)):
+        quarters = [(q // 2, slice(256 * (q % 2), 256 * (q % 2) + 256)) for q in range(4)]
+
+        def noise_of(q):
+            h, part = quarters[q]
             nc.vector.tensor_tensor(
-                out=noise[:, h, part],
-                in0=dev[:, h, part],
-                in1=eps_t[:, 512 * h + part.start : 512 * h + part.stop],
-                op=MULT,
+                out=noise[:, h, part], in0=dev[:, h, part], in1=eps_t[:, 256 * q : 256 * q + 256], op=MULT
             )
 
-        def sample(h):
+        def sample(q):
+            h, part = quarters[q]
             nc.vector.scalar_tensor_tensor(
-                out=z_t[:, h, :], in0=heads[0][h][:], scalar=rs[0][:], in1=noise[:, h, :], op0=MULT, op1=ADD
+                out=z_t[:, h, part], in0=heads[0][h][:, part], scalar=rs[0][:], in1=noise[:, h, part], op0=MULT, op1=ADD
             )
 
-        for h, part in ((0, slice(0, 256)), (0, slice(256, 512)), (1, slice(0, 512))):
+        for h, part in quarters:
             nc.scalar.activation(
                 out=dev[:, h, part], in_=heads[1][h][:, part], func=ACT.Exp, bias=nb[1][:], scale=half_rs[:]
             )
-        noise_of(0, slice(0, 256))
-        noise_of(0, slice(256, 512))
+        noise_of(0)
+        nc.vector.scalar_tensor_tensor(
+            out=nb[0][:], in0=mv[0][:, 0:1], scalar=-1.0, in1=rs[0][:], op0=MULT, op1=MULT
+        )
+        noise_of(1)
         sample(0)
+        sample(1)
+        nc.scalar.activation(
+            out=junk[:], in_=z_t[:, 0, :], func=ACT.Square, bias=nb[0][:], accum_out=sums[:, 1:2]
+        )
         nc.scalar.activation(
             out=zf_t[:, 0, :], in_=z_t[:, 0, :], func=ACT.Identity, bias=nb[0][:], accum_out=sums[:, 0:1]
         )
-        noise_of(1)
-        nc.scalar.activation(out=junk[:], in_=zf_t[:, 0, :], func=ACT.Square, accum_out=sums[:, 1:2])
+        noise_of(2)
+        noise_of(3)
+        sample(2)
+        sample(3)
         z_bank[0] = turn_back(zf_t, 0, "xt0")
-        sample(1)
         nc.scalar.activation(out=zf_t[:, 1, :], in_=z_t[:, 1, :], func=ACT.Identity, bias=nb[0][:])
         z_bank[1] = turn_back(zf_t, 1, "xt1")
+        nc.vector.bn_stats(out=trip[:, 6:12], in_=z_t[:, 1, 0:256])
+        nc.vector.tensor_scalar(out=nmean[:], in0=sums[:, 0:1], scalar1=-1.0 / 512, scalar2=None, op0=MULT)
         nc.vector.tensor_scalar(
             out=trip[:, 1:2], in0=sums[:, 0:1], scalar1=1.0 / 512, scalar2=nb[0][:], op0=MULT, op1=SUB
         )
-        nc.vector.tensor_scalar(out=nmean[:], in0=sums[:, 0:1], scalar1=-1.0 / 512, scalar2=None, op0=MULT)
-        nc.vector.bn_stats(out=trip[:, 6:12], in_=z_t[:, 1, :])
+        nc.vector.bn_stats(out=trip[:, 12:18], in_=z_t[:, 1, 256:512])
         nc.vector.scalar_tensor_tensor(
             out=trip[:, 2:3], in0=sums[:, 0:1], scalar=nmean[:], in1=sums[:, 1:2], op0=MULT, op1=ADD
         )

@@ -40,13 +40,13 @@ def tile_modelvd_pa_kernel(tc, en1_bytes, en1_scale, w2, b2, w_mean, w_logvar, e
         x_bytes = []
         w_raw = []
         for c in range(4):
+            xb = keep.tile([P, 2, K1], U8, name="xb%d" % c, align_bytes=64)
+            nc.sync.dma_start(out=xb[:], in_=x_rows[:, 2 * c : 2 * c + 2, :])
+            x_bytes.append(xb)
             if c < PASSES:
                 wr = keep.tile([P, 4, K2], BF16, name="wr%d" % c, align_bytes=64)
                 nc.sync.dma_start(out=wr[:], in_=w2[512 * c : 512 * c + 512, :].rearrange("(p j) c -> p j c", j=4))
                 w_raw.append(wr)
-            xb = keep.tile([P, 2, K1], U8, name="xb%d" % c, align_bytes=64)
-            nc.sync.dma_start(out=xb[:], in_=x_rows[:, 2 * c : 2 * c + 2, :])
-            x_bytes.append(xb)
         b2_raw = keep.tile([P, 4], BF16, name="b2_raw")
         nc.sync.dma_start(out=b2_raw[:], in_=b2.rearrange("(p t) -> p t", t=4))
         l_raw = keep.tile([P, 2, 4, D], BF16, name="l_raw", align_bytes=64)
@@ -55,14 +55,12 @@ def tile_modelvd_pa_kernel(tc, en1_bytes, en1_scale, w2, b2, w_mean, w_logvar, e
         eps_raw = keep.tile([P, TILES, D], BF16, name="eps_raw", align_bytes=64)
         nc.sync.dma_start(out=eps_raw[:], in_=eps.rearrange("(p i) d -> p i d", i=TILES))
 
-        trip = keep.tile([P, 18], F32, name="trip")
-        nc.vector.memset(trip[:], 0.0)
-        nc.vector.memset(trip[:, 0:1], 512.0)
-        nc.vector.memset(trip[:, 5:6], ROWS * BN_EPS)
         stats = [keep.tile([P, 21], F32, name="stats%d" % w) for w in range(2)]
-        for w in range(2):
-            nc.vector.memset(stats[w][:, 18:20], 0.0)
-            nc.vector.memset(stats[w][:, 20:21], ROWS * BN_EPS)
+        stats_z = keep.tile([P, 15], F32, name="stats_z")
+        for st in (stats[0], stats[1], stats_z):
+            n = st.shape[1]
+            nc.vector.memset(st[:, n - 3 : n - 1], 0.0)
+            nc.vector.memset(st[:, n - 1 : n], ROWS * BN_EPS)
         warm = keep.tile([P, 1], F32, name="warm")
         nc.vector.memset(warm[:], 0.0)
         warm_out = keep.tile([P, 1], F32, name="warm_out")
@@ -80,10 +78,12 @@ def tile_modelvd_pa_kernel(tc, en1_bytes, en1_scale, w2, b2, w_mean, w_logvar, e
             for t in range(4):
                 nc.tensor.transpose(st[:, t, :], scale_k[:, g, t : t + 1].to_broadcast([P, P]), ident_f[:])
             copy = (nc.vector.tensor_copy, nc.scalar.copy)[g]
-            copy(
-                out=scale_bc[:, 512 * g : 512 * (g + 1)].rearrange("p (m t) -> p m t", t=4),
-                in_=st[:].rearrange("p t m -> p m t"),
-            )
+            width = (P // 2, P)[g]
+            for m in range(0, P, width):
+                copy(
+                    out=scale_bc[:, 512 * g + 4 * m : 512 * g + 4 * (m + width)].rearrange("p (m t) -> p m t", t=4),
+                    in_=st[:, :, m : m + width].rearrange("p t m -> p m t"),
+                )
         b2_col = keep.tile([P, 4], F32, name="b2_col")
 
         prod = {}
@@ -99,8 +99,7 @@ def tile_modelvd_pa_kernel(tc, en1_bytes, en1_scale, w2, b2, w_mean, w_logvar, e
         def product(i):
             t = ring.tile([P, K1], BF16, name="prod", align_bytes=64)
             prod[i] = t
-            width = 512 if i == 0 else K1
-            for k in range(0, K1, width):
+            for k, width in ((0, 256), (256, 256), (512, 512)) if i == 0 else ((0, K1),):
                 ks = slice(k, k + width)
                 nc.vector.tensor_tensor(
                     out=t[:, ks], in0=x_bytes[i // 2][:, i % 2, ks].bitcast(FP8), in1=scale_bc[:, ks], op=MULT
@@ -146,14 +145,11 @@ def tile_modelvd_pa_kernel(tc, en1_bytes, en1_scale, w2, b2, w_mean, w_logvar, e
             w_planes.append(keep.tile([P, K2], U8, name="ws%d" % g, align_bytes=64))
 
         def weave_w(g, half):
-            src = w_raw[g][:].rearrange("p j (m t) -> p t m j", t=4)
-            ts = slice(2 * half, 2 * half + 2)
-            if (g, half) == (0, 0):
-                nc.gpsimd.tensor_scalar(
-                    out=w_grp[g][:, ts, :, :], in0=src[:, ts, :, :], scalar1=1.0, scalar2=0.0, op0=MULT, op1=ADD
-                )
-            else:
-                nc.scalar.copy(out=w_grp[g][:, ts, :, :], in_=src[:, ts, :, :])
+            ms = slice(64 * half, 64 * half + 64)
+            nc.scalar.copy(
+                out=w_grp[g][:].rearrange("p t m j -> p m j t")[:, ms, :, :],
+                in_=w_raw[g][:].rearrange("p j (m t) -> p m j t", t=4)[:, ms, :, :],
+            )
 
         def quant_w(g):
             nc.vector.quantize_mx(
@@ -167,7 +163,11 @@ def tile_modelvd_pa_kernel(tc, en1_bytes, en1_scale, w2, b2, w_mean, w_logvar, e
         l_planes = keep.tile([P, 2 * D], U8, name="l_planes", align_bytes=64)
 
         def weave_l():
-            nc.scalar.copy(out=l_grp[:], in_=l_raw[:].rearrange("p w j n -> p w n j"))
+            for w in range(2):
+                nc.scalar.copy(
+                    out=l_grp[:, w, :, :].rearrange("p (c i) j -> p c j i", i=4),
+                    in_=l_raw[:, w, :, :].rearrange("p j (c i) -> p c j i", i=4),
+                )
 
         def quant_l():
             nc.vector.quantize_mx(
@@ -210,23 +210,9 @@ def tile_modelvd_pa_kernel(tc, en1_bytes, en1_scale, w2, b2, w_mean, w_logvar, e
                     out=hidden[c][:, t, :], in_=acc[c, t // 2][:, t % 2, :], func=ACT.Relu, bias=b2_col[:, t : t + 1]
                 )
 
-        def add_b2(c):
-            hg = ring.tile([P, P, 4], BF16, name="hg", align_bytes=64)
-            h_grp[c] = hg
-            nc.vector.tensor_tensor(
-                out=hg[:],
-                in0=acc[c, 0][:].rearrange("p t n -> p n t"),
-                in1=b2_col[:].unsqueeze(1).to_broadcast([P, P, 4]),
-                op=ADD,
-            )
-
-        def relu_in_place(c):
-            nc.scalar.activation(out=h_grp[c][:], in_=h_grp[c][:], func=ACT.Relu)
-
         def relu_v(c, ts):
-            n = CHUNKS[c][1] * P
             if c not in hidden:
-                h = ring.tile([P, 4, n], BF16, name="hid", align_bytes=64)
+                h = ring.tile([P, 4, CHUNKS[c][1] * P], BF16, name="hid", align_bytes=64)
                 hidden[c] = h
             for t in ts:
                 nc.vector.tensor_scalar(
@@ -238,6 +224,24 @@ def tile_modelvd_pa_kernel(tc, en1_bytes, en1_scale, w2, b2, w_mean, w_logvar, e
                     op1=mybir.AluOpType.max,
                 )
 
+        def add_b2(c):
+            hg = ring.tile([P, P, 4], BF16, name="hg", align_bytes=64)
+            h_grp[c] = hg
+            nc.vector.tensor_tensor(
+                out=hg[:],
+                in0=acc[c, 0][:].rearrange("p t n -> p n t"),
+                in1=b2_col[:].unsqueeze(1).to_broadcast([P, P, 4]),
+                op=ADD,
+            )
+
+        def relu_in_place(c):
+            if c == 3:
+                nc.scalar.activation(out=h_grp[c][:], in_=h_grp[c][:], func=ACT.Relu)
+            else:
+                nc.vector.tensor_scalar(
+                    out=h_grp[c][:], in0=h_grp[c][:], scalar1=0.0, scalar2=None, op0=mybir.AluOpType.max
+                )
+
         h_codes = {}
         h_planes = {}
 
@@ -247,7 +251,7 @@ def tile_modelvd_pa_kernel(tc, en1_bytes, en1_scale, w2, b2, w_mean, w_logvar, e
             h_grp[c] = hg
             dst = hg[:].rearrange("p (c i) t -> p c t i", i=4)
             src = hidden[c][:].rearrange("p t (c i) -> p c t i", i=4)
-            if c != 1:
+            if c == 2:
                 nc.scalar.copy(out=dst, in_=src)
             else:
                 nc.vector.tensor_copy(out=dst, in_=src)
@@ -290,7 +294,6 @@ def tile_modelvd_pa_kernel(tc, en1_bytes, en1_scale, w2, b2, w_mean, w_logvar, e
                 nc.vector.bn_stats(out=stats[w][:, 6 * part : 6 * part + 6], in_=heads[w][h][:, cols])
 
         eps_bank = []
-        eps_t = keep.tile([P, ROWS], BF16, name="eps_t", align_bytes=64)
 
         def turn_eps():
             et = psum.tile([P, TILES, P], BF16, name="xt0")
@@ -298,193 +301,158 @@ def tile_modelvd_pa_kernel(tc, en1_bytes, en1_scale, w2, b2, w_mean, w_logvar, e
                 nc.tensor.transpose(et[:, i, :], eps_raw[:, i, :], ident_b[:])
             eps_bank.append(et)
 
-        def empty_eps():
-            nc.scalar.copy(out=eps_t[:], in_=eps_bank[0][:].rearrange("p i r -> p (i r)"))
-
-        weave_w(0, 0)
         nc.gpsimd.tensor_copy(out=b2_col[:], in_=b2_raw[:])
         product(0)
+        weave_w(0, 0)
+        product(1)
         weave_w(0, 1)
         turn(0)
-        product(1)
-        weave_w(1, 0)
         product(2)
         turn(1)
         empty(0)
-        weave_w(1, 1)
-        quant_w(0)
-        turn(2)
+        weave_w(1, 0)
         product(3)
+        turn(2)
+        product(4)
+        weave_w(1, 1)
+        turn(3)
+        quant_w(0)
         empty(1)
+        turn(4)
         quant_w(1)
         empty(2)
-        turn(3)
-        weave_l()
         quant_x(0)
-        product(4)
-        mm1(0, 0)
         empty(3)
-        mm1(0, 1)
         product(5)
-        relu(0, (0, 1))
-        turn(4)
-        relu(0, (3,))
+        weave_l()
+        mm1(0, 0)
+        mm1(0, 1)
         quant_x(1)
         empty(4)
         turn(5)
+        relu_v(0, (0,))
+        relu(0, (1,))
         product(6)
         relu(0, (2,))
         mm1(1, 0)
+        relu(0, (3,))
         empty(5)
-        weave_h(0)
-        mm1(1, 1)
-        quant_l()
-        quant_x(2)
-        turn(6)
-        relu_v(1, (0,))
-        turn_eps()
-        relu(1, (1,))
         product(7)
-        empty(6)
-        mm1(2, 0)
-        relu(1, (2, 3))
-        quant_x(3)
+        mm1(1, 1)
+        relu(1, (1,))
+        turn(6)
+        relu(1, (0,))
+        relu(1, (3,))
+        quant_x(2)
+        relu(1, (2,))
         turn(7)
-        quant_h(0)
-        relu(2, (0, 1))
-        weave_h(1)
-        mm1(2, 1)
+        empty(6)
+        weave_h(0)
+        mm1(2, 0)
         empty(7)
-        mm1(3, 0)
-        quant_h(1)
-        relu(2, (2, 3))
+        quant_x(3)
+        mm1(2, 1)
+        turn_eps()
+        weave_h(1)
+        relu(2, (1,))
+        relu(2, (0,))
         quant_x(4)
-        mm2(0)
-        mm2(1)
-        add_b2(3)
-        mm1(4, 0)
+        relu(2, (2,))
+        quant_h(0)
+        mm1(3, 0)
+        relu(2, (3,))
+        quant_l()
+        quant_h(1)
         weave_h(2)
-        stat(0, (1,))
+        mm1(4, 0)
+        add_b2(3)
+        mm2(1)
         add_b2(4)
+        mm2(0)
         relu_in_place(3)
         quant_h(2)
         relu_in_place(4)
-        mm2(2)
         quant_h(3)
-        stat(0, (0,))
-        empty_eps()
+        mm2(2)
         mm2(3)
         quant_h(4)
         mm2(4)
-        stat(1, (1,))
 
         mv = [keep.tile([P, 2], F32, name="mv%d" % w) for w in range(2)]
         rs = [keep.tile([P, 1], F32, name="rs%d" % w) for w in range(2)]
         nb = [keep.tile([P, 1], F32, name="nb%d" % w) for w in range(2)]
         half_rs = keep.tile([P, 1], F32, name="half_rs")
-        stat(2, (1,))
+        for part in range(3):
+            stat(part, (1,))
         nc.vector.bn_aggr(out=mv[1][:], in_=stats[1][:])
         nc.gpsimd.tensor_tensor(out=rs[1][:], in0=mv[1][:, 1:2], in1=neg_half[:], op=POW)
-        stat(1, (0,))
+        for part in range(3):
+            stat(part, (0,))
         nc.vector.scalar_tensor_tensor(
             out=nb[1][:], in0=mv[1][:, 0:1], scalar=-0.5, in1=rs[1][:], op0=MULT, op1=MULT
         )
         nc.vector.tensor_scalar(out=half_rs[:], in0=rs[1][:], scalar1=0.5, scalar2=None, op0=MULT)
-        stat(2, (0,))
         nc.vector.bn_aggr(out=mv[0][:], in_=stats[0][:])
         nc.gpsimd.tensor_tensor(out=rs[0][:], in0=mv[0][:, 1:2], in1=neg_half[:], op=POW)
+
         dev = keep.tile([P, 2, 512], F32, name="dev", align_bytes=64)
         noise = keep.tile([P, 2, 512], F32, name="noise", align_bytes=64)
         z_t = keep.tile([P, 2, 512], F32, name="z_t", align_bytes=64)
         zf_t = keep.tile([P, 2, 512], F32, name="zf_t", align_bytes=64)
         zx_t = keep.tile([P, 2, 512], F32, name="zx_t", align_bytes=64)
-        junk = keep.tile([P, 512], F32, name="junk", align_bytes=64)
-        sums = keep.tile([P, 2], F32, name="sums")
-        nmean = keep.tile([P, 1], F32, name="nmean")
-
-        z_bank = {}
-
-        def turn_back(src, h, name):
-            b = psum.tile([P, 4, P], F32, name=name)
-            for i in range(4):
-                nc.tensor.transpose(b[:, i, :], src[:, h, P * i : P * i + P], ident_f[:])
-            return b
-
         quarters = [(q // 2, slice(256 * (q % 2), 256 * (q % 2) + 256)) for q in range(4)]
-
-        def noise_of(q):
-            h, part = quarters[q]
-            nc.vector.tensor_tensor(
-                out=noise[:, h, part], in0=dev[:, h, part], in1=eps_t[:, 256 * q : 256 * q + 256], op=MULT
-            )
-
-        def sample(q):
-            h, part = quarters[q]
-            nc.vector.scalar_tensor_tensor(
-                out=z_t[:, h, part], in0=heads[0][h][:, part], scalar=rs[0][:], in1=noise[:, h, part], op0=MULT, op1=ADD
-            )
-
         for h, part in quarters:
             nc.scalar.activation(
                 out=dev[:, h, part], in_=heads[1][h][:, part], func=ACT.Exp, bias=nb[1][:], scale=half_rs[:]
             )
-        noise_of(0)
+        nc.scalar.activation(out=warm_out[:], in_=mv[1][:, 1:2], func=ACT.Abs_reciprocal_sqrt)
+        for q, (h, part) in enumerate(quarters):
+            nc.vector.tensor_tensor(
+                out=noise[:, h, part],
+                in0=dev[:, h, part],
+                in1=eps_bank[0][:, 2 * q : 2 * q + 2, :].rearrange("p i r -> p (i r)"),
+                op=MULT,
+            )
         nc.vector.scalar_tensor_tensor(
             out=nb[0][:], in0=mv[0][:, 0:1], scalar=-1.0, in1=rs[0][:], op0=MULT, op1=MULT
         )
-        noise_of(1)
-        sample(0)
-        sample(1)
-        nc.scalar.activation(
-            out=junk[:], in_=z_t[:, 0, :], func=ACT.Square, bias=nb[0][:], accum_out=sums[:, 1:2]
-        )
-        nc.scalar.activation(
-            out=zf_t[:, 0, :], in_=z_t[:, 0, :], func=ACT.Identity, bias=nb[0][:], accum_out=sums[:, 0:1]
-        )
-        noise_of(2)
-        noise_of(3)
-        sample(2)
-        sample(3)
-        z_bank[0] = turn_back(zf_t, 0, "xt0")
-        nc.scalar.activation(out=zf_t[:, 1, :], in_=z_t[:, 1, :], func=ACT.Identity, bias=nb[0][:])
-        z_bank[1] = turn_back(zf_t, 1, "xt1")
-        nc.vector.bn_stats(out=trip[:, 6:12], in_=z_t[:, 1, 0:256])
-        nc.vector.tensor_scalar(out=nmean[:], in0=sums[:, 0:1], scalar1=-1.0 / 512, scalar2=None, op0=MULT)
-        nc.vector.tensor_scalar(
-            out=trip[:, 1:2], in0=sums[:, 0:1], scalar1=1.0 / 512, scalar2=nb[0][:], op0=MULT, op1=SUB
-        )
-        nc.vector.bn_stats(out=trip[:, 12:18], in_=z_t[:, 1, 256:512])
-        nc.vector.scalar_tensor_tensor(
-            out=trip[:, 2:3], in0=sums[:, 0:1], scalar=nmean[:], in1=sums[:, 1:2], op0=MULT, op1=ADD
-        )
+        for h, part in quarters:
+            nc.vector.scalar_tensor_tensor(
+                out=z_t[:, h, part], in0=heads[0][h][:, part], scalar=rs[0][:], in1=noise[:, h, part], op0=MULT, op1=ADD
+            )
+        z_bank = []
+        for h in range(2):
+            nc.vector.bn_stats(out=stats_z[:, 6 * h : 6 * h + 6], in_=z_t[:, h, :])
+            nc.scalar.activation(out=zf_t[:, h, :], in_=z_t[:, h, :], func=ACT.Identity, bias=nb[0][:])
+            b = psum.tile([P, 4, P], F32, name=("xt1", "acc0")[h])
+            for i in range(4):
+                nc.tensor.transpose(b[:, i, :], zf_t[:, h, P * i : P * i + P], ident_f[:])
+            z_bank.append(b)
         mvz = keep.tile([P, 2], F32, name="mvz")
         rsz = keep.tile([P, 1], F32, name="rsz")
-        nc.vector.bn_aggr(out=mvz[:], in_=trip[:])
-        nc.gpsimd.tensor_tensor(out=rsz[:], in0=mvz[:, 1:2], in1=neg_half[:], op=POW)
+        nc.vector.bn_aggr(out=mvz[:], in_=stats_z[:])
+        nc.scalar.activation(out=rsz[:], in_=mvz[:, 1:2], func=ACT.Abs_reciprocal_sqrt)
 
         z_out = keep.tile([P, TILES, P], F32, name="z_out", align_bytes=64)
         zx_out = keep.tile([P, TILES, P], F32, name="zx_out", align_bytes=64)
         z_rows = out_z.rearrange("(p i) d -> p i d", i=TILES)
-        zx_bank = []
         zx_rows = out_zx.rearrange("(p i) d -> p i d", i=TILES)
-        for h in range(2):
-            cols = slice(4 * h, 4 * h + 4)
-            nc.scalar.copy(out=z_out[:, cols, :], in_=z_bank[h][:])
-            nc.sync.dma_start(out=z_rows[:, cols, :], in_=z_out[:, cols, :])
-        for q in range(4):
-            cols = slice(2 * q, 2 * q + 2)
-            part = slice(256 * (q % 2), 256 * (q % 2) + 256)
+        nc.vector.tensor_copy(out=z_out[:, 0:2, :], in_=z_bank[0][:, 0:2, :])
+        nc.scalar.copy(out=z_out[:, 4:8, :], in_=z_bank[1][:])
+        nc.sync.dma_start(out=z_rows[:, 4:8, :], in_=z_out[:, 4:8, :])
+        nc.scalar.copy(out=z_out[:, 2:4, :], in_=z_bank[0][:, 2:4, :])
+        nc.sync.dma_start(out=z_rows[:, 0:4, :], in_=z_out[:, 0:4, :])
+        zx_bank = []
+        for q, (h, part) in enumerate(quarters):
             nc.vector.tensor_scalar(
-                out=zx_t[:, q // 2, part], in0=z_t[:, q // 2, part], scalar1=mvz[:, 0:1], scalar2=rsz[:], op0=SUB, op1=MULT
+                out=zx_t[:, h, part], in0=z_t[:, h, part], scalar1=mvz[:, 0:1], scalar2=rsz[:], op0=SUB, op1=MULT
             )
-            b = psum.tile([P, 2, P], F32, name=("acc0", "acc1", "head10", "head11")[q])
+            b = psum.tile([P, 2, P], F32, name=("acc1", "head10", "head11", "xt0")[q])
             for i in range(2):
-                nc.tensor.transpose(b[:, i, :], zx_t[:, q // 2, 256 * (q % 2) + P * i : 256 * (q % 2) + P * i + P], ident_f[:])
+                nc.tensor.transpose(b[:, i, :], zx_t[:, h, part.start + P * i : part.start + P * i + P], ident_f[:])
             zx_bank.append(b)
         for q in range(4):
             cols = slice(2 * q, 2 * q + 2)
-            if q % 2 == 0:
-                nc.scalar.copy(out=zx_out[:, cols, :], in_=zx_bank[q][:])
-            else:
-                nc.vector.tensor_copy(out=zx_out[:, cols, :], in_=zx_bank[q][:])
+            copy = (nc.scalar.copy, nc.vector.tensor_copy)[q % 2]
+            copy(out=zx_out[:, cols, :], in_=zx_bank[q][:])
             nc.sync.dma_start(out=zx_rows[:, cols, :], in_=zx_out[:, cols, :])

@@ -34,8 +34,11 @@ def tile_modelvd_pa_kernel(tc, en1_bytes, en1_scale, w2, b2, w_mean, w_logvar, e
         psum = ctx.enter_context(tc.psum_pool(name="psum", bufs=1))
         ctx.enter_context(tc.manual_schedule())
 
-        scale_k = keep.tile([P, PASSES, 4], F32, name="scale_k")
-        nc.sync.dma_start(out=scale_k[:], in_=en1_scale.rearrange("o (g p t) -> p (o g) t", p=P, t=4))
+        scale_k = []
+        for g in range(PASSES):
+            sk = keep.tile([P, 4], F32, name="scale_k%d" % g)
+            nc.sync.dma_start(out=sk[:], in_=en1_scale[:, 512 * g : 512 * (g + 1)].rearrange("o (p t) -> p (o t)", t=4))
+            scale_k.append(sk)
         x_rows = en1_bytes.rearrange("(p i) k -> p i k", i=TILES)
         x_bytes = []
         w_raw = []
@@ -76,7 +79,7 @@ def tile_modelvd_pa_kernel(tc, en1_bytes, en1_scale, w2, b2, w_mean, w_logvar, e
         for g in range(PASSES):
             st = psum.tile([P, 4, P], F32, name="xt%d" % g)
             for t in range(4):
-                nc.tensor.transpose(st[:, t, :], scale_k[:, g, t : t + 1].to_broadcast([P, P]), ident_f[:])
+                nc.tensor.transpose(st[:, t, :], scale_k[g][:, t : t + 1].to_broadcast([P, P]), ident_f[:])
             copy = (nc.vector.tensor_copy, nc.scalar.copy)[g]
             width = (P // 2, P)[g]
             for m in range(0, P, width):
@@ -84,7 +87,6 @@ def tile_modelvd_pa_kernel(tc, en1_bytes, en1_scale, w2, b2, w_mean, w_logvar, e
                     out=scale_bc[:, 512 * g + 4 * m : 512 * g + 4 * (m + width)].rearrange("p (m t) -> p m t", t=4),
                     in_=st[:, :, m : m + width].rearrange("p t m -> p m t"),
                 )
-        b2_col = keep.tile([P, 4], F32, name="b2_col")
 
         prod = {}
         turned = {}
@@ -96,14 +98,13 @@ def tile_modelvd_pa_kernel(tc, en1_bytes, en1_scale, w2, b2, w_mean, w_logvar, e
             for ii in range(count):
                 where[first + ii] = (c, ii)
 
-        def product(i):
-            t = ring.tile([P, K1], BF16, name="prod", align_bytes=64)
-            prod[i] = t
-            for k, width in ((0, 256), (256, 256), (512, 512)) if i == 0 else ((0, K1),):
-                ks = slice(k, k + width)
-                nc.vector.tensor_tensor(
-                    out=t[:, ks], in0=x_bytes[i // 2][:, i % 2, ks].bitcast(FP8), in1=scale_bc[:, ks], op=MULT
-                )
+        def product(i, ks=slice(0, K1)):
+            if i not in prod:
+                t = ring.tile([P, K1], BF16, name="prod", align_bytes=64)
+                prod[i] = t
+            nc.vector.tensor_tensor(
+                out=prod[i][:, ks], in0=x_bytes[i // 2][:, i % 2, ks].bitcast(FP8), in1=scale_bc[:, ks], op=MULT
+            )
 
         def turn(i):
             xt = psum.tile([P, PASSES, 2, P], F32, name=("xt0", "xt1", "head01", "head11")[i % 4])
@@ -162,12 +163,11 @@ def tile_modelvd_pa_kernel(tc, en1_bytes, en1_scale, w2, b2, w_mean, w_logvar, e
         l_codes = keep.tile([P, 2 * D], U32, name="l_codes", align_bytes=64)
         l_planes = keep.tile([P, 2 * D], U8, name="l_planes", align_bytes=64)
 
-        def weave_l():
-            for w in range(2):
-                nc.scalar.copy(
-                    out=l_grp[:, w, :, :].rearrange("p (c i) j -> p c j i", i=4),
-                    in_=l_raw[:, w, :, :].rearrange("p j (c i) -> p c j i", i=4),
-                )
+        def weave_l(w):
+            nc.scalar.copy(
+                out=l_grp[:, w, :, :].rearrange("p (c i) j -> p c j i", i=4),
+                in_=l_raw[:, w, :, :].rearrange("p j (c i) -> p c j i", i=4),
+            )
 
         def quant_l():
             nc.vector.quantize_mx(
@@ -179,7 +179,7 @@ def tile_modelvd_pa_kernel(tc, en1_bytes, en1_scale, w2, b2, w_mean, w_logvar, e
         def mm1(c, pair):
             n = CHUNKS[c][1] * P
             if c in ADDED:
-                a = psum.tile([P, 4, n], F32, name="acc%d" % ((c + 1) % 2))
+                a = psum.tile([P, 4, n], F32, name=("xt1", "acc0")[c - 3])
             else:
                 a = psum.tile([P, 2, n], F32, name="acc%d" % pair)
             if True:
@@ -207,21 +207,7 @@ def tile_modelvd_pa_kernel(tc, en1_bytes, en1_scale, w2, b2, w_mean, w_logvar, e
                 hidden[c] = h
             for t in ts:
                 nc.scalar.activation(
-                    out=hidden[c][:, t, :], in_=acc[c, t // 2][:, t % 2, :], func=ACT.Relu, bias=b2_col[:, t : t + 1]
-                )
-
-        def relu_v(c, ts):
-            if c not in hidden:
-                h = ring.tile([P, 4, CHUNKS[c][1] * P], BF16, name="hid", align_bytes=64)
-                hidden[c] = h
-            for t in ts:
-                nc.vector.tensor_scalar(
-                    out=hidden[c][:, t, :],
-                    in0=acc[c, t // 2][:, t % 2, :],
-                    scalar1=b2_col[:, t : t + 1],
-                    scalar2=0.0,
-                    op0=ADD,
-                    op1=mybir.AluOpType.max,
+                    out=hidden[c][:, t, :], in_=acc[c, t // 2][:, t % 2, :], func=ACT.Relu, bias=b2_raw[:, t : t + 1]
                 )
 
         def add_b2(c):
@@ -230,7 +216,7 @@ def tile_modelvd_pa_kernel(tc, en1_bytes, en1_scale, w2, b2, w_mean, w_logvar, e
             nc.vector.tensor_tensor(
                 out=hg[:],
                 in0=acc[c, 0][:].rearrange("p t n -> p n t"),
-                in1=b2_col[:].unsqueeze(1).to_broadcast([P, P, 4]),
+                in1=b2_raw[:].unsqueeze(1).to_broadcast([P, P, 4]),
                 op=ADD,
             )
 
@@ -301,91 +287,98 @@ def tile_modelvd_pa_kernel(tc, en1_bytes, en1_scale, w2, b2, w_mean, w_logvar, e
                 nc.tensor.transpose(et[:, i, :], eps_raw[:, i, :], ident_b[:])
             eps_bank.append(et)
 
-        nc.gpsimd.tensor_copy(out=b2_col[:], in_=b2_raw[:])
-        product(0)
+        product(0, slice(0, 256))
+        product(0, slice(256, 512))
         weave_w(0, 0)
-        product(1)
+        product(1, slice(0, 512))
+        product(0, slice(512, K1))
         weave_w(0, 1)
+        product(1, slice(512, K1))
         turn(0)
         product(2)
         turn(1)
-        empty(0)
         weave_w(1, 0)
         product(3)
         turn(2)
-        product(4)
-        weave_w(1, 1)
-        turn(3)
-        quant_w(0)
+        empty(0)
         empty(1)
+        product(4)
+        turn(3)
+        weave_w(1, 1)
+        quant_w(0)
         turn(4)
-        quant_w(1)
-        empty(2)
+        weave_l(0)
         quant_x(0)
+        empty(2)
+        quant_w(1)
         empty(3)
         product(5)
-        weave_l()
         mm1(0, 0)
-        mm1(0, 1)
-        quant_x(1)
         empty(4)
-        turn(5)
-        relu_v(0, (0,))
+        mm1(0, 1)
         relu(0, (1,))
-        product(6)
+        quant_x(1)
+        relu(0, (0,))
+        turn(5)
         relu(0, (2,))
+        product(6)
         mm1(1, 0)
         relu(0, (3,))
-        empty(5)
-        product(7)
+        weave_l(1)
         mm1(1, 1)
-        relu(1, (1,))
+        product(7)
+        empty(5)
         turn(6)
         relu(1, (0,))
-        relu(1, (3,))
-        quant_x(2)
         relu(1, (2,))
+        quant_x(2)
+        relu(1, (1,))
         turn(7)
-        empty(6)
+        relu(1, (3,))
         weave_h(0)
+        empty(6)
         mm1(2, 0)
+        quant_l()
         empty(7)
-        quant_x(3)
         mm1(2, 1)
-        turn_eps()
-        weave_h(1)
+        quant_x(3)
         relu(2, (1,))
+        quant_h(0)
+        mm1(3, 0)
         relu(2, (0,))
         quant_x(4)
         relu(2, (2,))
-        quant_h(0)
-        mm1(3, 0)
-        relu(2, (3,))
-        quant_l()
-        quant_h(1)
-        weave_h(2)
+        weave_h(1)
         mm1(4, 0)
+        relu(2, (3,))
         add_b2(3)
-        mm2(1)
-        add_b2(4)
+        weave_h(2)
         mm2(0)
+        turn_eps()
+        add_b2(4)
+        quant_h(1)
         relu_in_place(3)
-        quant_h(2)
         relu_in_place(4)
-        quant_h(3)
-        mm2(2)
-        mm2(3)
+        mm2(1)
+        quant_h(2)
         quant_h(4)
+        mm2(2)
+        quant_h(3)
         mm2(4)
+        mm2(3)
 
         mv = [keep.tile([P, 2], F32, name="mv%d" % w) for w in range(2)]
         rs = [keep.tile([P, 1], F32, name="rs%d" % w) for w in range(2)]
         nb = [keep.tile([P, 1], F32, name="nb%d" % w) for w in range(2)]
         half_rs = keep.tile([P, 1], F32, name="half_rs")
-        for part in range(3):
+        half_nm = keep.tile([P, 1], F32, name="half_nm")
+        dev = keep.tile([P, 2, 512], F32, name="dev", align_bytes=64)
+        for part in (0, 2, 1):
             stat(part, (1,))
         nc.vector.bn_aggr(out=mv[1][:], in_=stats[1][:])
         nc.gpsimd.tensor_tensor(out=rs[1][:], in0=mv[1][:, 1:2], in1=neg_half[:], op=POW)
+        nc.vector.tensor_scalar(out=half_nm[:], in0=mv[1][:, 0:1], scalar1=-0.5, scalar2=None, op0=MULT)
+        nc.scalar.activation(out=dev[:, 0, :], in_=heads[1][0][:], func=ACT.Identity, bias=half_nm[:], scale=0.5)
         for part in range(3):
             stat(part, (0,))
         nc.vector.scalar_tensor_tensor(
@@ -395,16 +388,24 @@ def tile_modelvd_pa_kernel(tc, en1_bytes, en1_scale, w2, b2, w_mean, w_logvar, e
         nc.vector.bn_aggr(out=mv[0][:], in_=stats[0][:])
         nc.gpsimd.tensor_tensor(out=rs[0][:], in0=mv[0][:, 1:2], in1=neg_half[:], op=POW)
 
-        dev = keep.tile([P, 2, 512], F32, name="dev", align_bytes=64)
         noise = keep.tile([P, 2, 512], F32, name="noise", align_bytes=64)
         z_t = keep.tile([P, 2, 512], F32, name="z_t", align_bytes=64)
         zf_t = keep.tile([P, 2, 512], F32, name="zf_t", align_bytes=64)
         zx_t = keep.tile([P, 2, 512], F32, name="zx_t", align_bytes=64)
+        def turn_back(src, h, part, name):
+            b = psum.tile([P, 2, P], F32, name=name)
+            for i in range(2):
+                nc.tensor.transpose(b[:, i, :], src[:, h, part.start + P * i : part.start + P * i + P], ident_f[:])
+            return b
+
         quarters = [(q // 2, slice(256 * (q % 2), 256 * (q % 2) + 256)) for q in range(4)]
         for h, part in quarters:
-            nc.scalar.activation(
-                out=dev[:, h, part], in_=heads[1][h][:, part], func=ACT.Exp, bias=nb[1][:], scale=half_rs[:]
-            )
+            if h == 0:
+                nc.scalar.activation(out=dev[:, h, part], in_=dev[:, h, part], func=ACT.Exp, scale=rs[1][:])
+            else:
+                nc.scalar.activation(
+                    out=dev[:, h, part], in_=heads[1][h][:, part], func=ACT.Exp, bias=nb[1][:], scale=half_rs[:]
+                )
         nc.scalar.activation(out=warm_out[:], in_=mv[1][:, 1:2], func=ACT.Abs_reciprocal_sqrt)
         for q, (h, part) in enumerate(quarters):
             nc.vector.tensor_tensor(
@@ -423,34 +424,28 @@ def tile_modelvd_pa_kernel(tc, en1_bytes, en1_scale, w2, b2, w_mean, w_logvar, e
         z_bank = []
         for h in range(2):
             nc.vector.bn_stats(out=stats_z[:, 6 * h : 6 * h + 6], in_=z_t[:, h, :])
-            nc.scalar.activation(out=zf_t[:, h, :], in_=z_t[:, h, :], func=ACT.Identity, bias=nb[0][:])
-            b = psum.tile([P, 4, P], F32, name=("xt1", "acc0")[h])
-            for i in range(4):
-                nc.tensor.transpose(b[:, i, :], zf_t[:, h, P * i : P * i + P], ident_f[:])
-            z_bank.append(b)
+        for q, (h, part) in enumerate(quarters):
+            nc.scalar.activation(out=zf_t[:, h, part], in_=z_t[:, h, part], func=ACT.Identity, bias=nb[0][:])
+            z_bank.append(turn_back(zf_t, h, part, ("xt1", "acc0", "acc1", "head10")[q]))
         mvz = keep.tile([P, 2], F32, name="mvz")
         rsz = keep.tile([P, 1], F32, name="rsz")
         nc.vector.bn_aggr(out=mvz[:], in_=stats_z[:])
-        nc.scalar.activation(out=rsz[:], in_=mvz[:, 1:2], func=ACT.Abs_reciprocal_sqrt)
-
         z_out = keep.tile([P, TILES, P], F32, name="z_out", align_bytes=64)
         zx_out = keep.tile([P, TILES, P], F32, name="zx_out", align_bytes=64)
         z_rows = out_z.rearrange("(p i) d -> p i d", i=TILES)
         zx_rows = out_zx.rearrange("(p i) d -> p i d", i=TILES)
-        nc.vector.tensor_copy(out=z_out[:, 0:2, :], in_=z_bank[0][:, 0:2, :])
-        nc.scalar.copy(out=z_out[:, 4:8, :], in_=z_bank[1][:])
-        nc.sync.dma_start(out=z_rows[:, 4:8, :], in_=z_out[:, 4:8, :])
-        nc.scalar.copy(out=z_out[:, 2:4, :], in_=z_bank[0][:, 2:4, :])
-        nc.sync.dma_start(out=z_rows[:, 0:4, :], in_=z_out[:, 0:4, :])
+        for q in range(4):
+            if q == 2:
+                nc.scalar.activation(out=rsz[:], in_=mvz[:, 1:2], func=ACT.Abs_reciprocal_sqrt)
+            nc.scalar.copy(out=z_out[:, 2 * q : 2 * q + 2, :], in_=z_bank[q][:])
+            if q % 2 == 1:
+                nc.sync.dma_start(out=z_rows[:, 2 * q - 2 : 2 * q + 2, :], in_=z_out[:, 2 * q - 2 : 2 * q + 2, :])
         zx_bank = []
         for q, (h, part) in enumerate(quarters):
             nc.vector.tensor_scalar(
                 out=zx_t[:, h, part], in0=z_t[:, h, part], scalar1=mvz[:, 0:1], scalar2=rsz[:], op0=SUB, op1=MULT
             )
-            b = psum.tile([P, 2, P], F32, name=("acc1", "head10", "head11", "xt0")[q])
-            for i in range(2):
-                nc.tensor.transpose(b[:, i, :], zx_t[:, h, part.start + P * i : part.start + P * i + P], ident_f[:])
-            zx_bank.append(b)
+            zx_bank.append(turn_back(zx_t, h, part, ("head11", "xt0", "xt1", "acc0")[q]))
         for q in range(4):
             cols = slice(2 * q, 2 * q + 2)
             copy = (nc.scalar.copy, nc.vector.tensor_copy)[q % 2]

from contextlib import ExitStack

import concourse.mybir as mybir
from concourse.masks import make_identity

F32 = mybir.dt.float32
BF16 = mybir.dt.bfloat16
U32 = mybir.dt.uint32
U8 = mybir.dt.uint8
FP8 = mybir.dt.float8_e4m3fn
FP8X4 = mybir.dt.float8_e4m3fn_x4
ADD = mybir.AluOpType.add
SUB = mybir.AluOpType.subtract
MULT = mybir.AluOpType.mult
POW = mybir.AluOpType.pow
ACT = mybir.ActivationFunctionType

P = 128
ROWS, K1, K2, D = 1024, 1024, 512, 128
TILES = ROWS // P
PASSES = K1 // 512
CHUNKS = [(0, 2), (2, 2), (4, 2), (6, 1), (7, 1)]
ADDED = (3, 4)
BN_EPS = 1e-5

FLOPS = 2 * ROWS * K1 * K2 + 2 * ROWS * K2 * D * 2


def tile_modelvd_pa_kernel(tc, en1_bytes, en1_scale, w2, b2, w_mean, w_logvar, eps, out_z, out_zx):
    nc = tc.nc
    with ExitStack() as ctx:
        keep = ctx.enter_context(tc.tile_pool(name="keep", bufs=1))
        ring = ctx.enter_context(tc.tile_pool(name="ring", bufs=6))
        psum = ctx.enter_context(tc.psum_pool(name="psum", bufs=1))
        ctx.enter_context(tc.manual_schedule())

        scale_k = []
        for g in range(PASSES):
            sk = keep.tile([P, 4], F32, name="scale_k%d" % g)
            nc.sync.dma_start(out=sk[:], in_=en1_scale[:, 512 * g : 512 * (g + 1)].rearrange("o (p t) -> p (o t)", t=4))
            scale_k.append(sk)
        x_rows = en1_bytes.rearrange("(p i) k -> p i k", i=TILES)
        x_bytes = []
        w_raw = []
        for c in range(4):
            xb = keep.tile([P, 2, K1], U8, name="xb%d" % c, align_bytes=64)
            nc.sync.dma_start(out=xb[:], in_=x_rows[:, 2 * c : 2 * c + 2, :])
            x_bytes.append(xb)
            if c < PASSES:
                wr = keep.tile([P, 4, K2], BF16, name="wr%d" % c, align_bytes=64)
                nc.sync.dma_start(out=wr[:], in_=w2[512 * c : 512 * c + 512, :].rearrange("(p j) c -> p j c", j=4))
                w_raw.append(wr)
        b2_raw = keep.tile([P, 4], BF16, name="b2_raw")
        nc.sync.dma_start(out=b2_raw[:], in_=b2.rearrange("(p t) -> p t", t=4))
        l_raw = keep.tile([P, 2, 4, D], BF16, name="l_raw", align_bytes=64)
        nc.sync.dma_start(out=l_raw[:, 0, :, :], in_=w_mean.rearrange("(p j) n -> p j n", j=4))
        nc.sync.dma_start(out=l_raw[:, 1, :, :], in_=w_logvar.rearrange("(p j) n -> p j n", j=4))
        eps_raw = keep.tile([P, TILES, D], BF16, name="eps_raw", align_bytes=64)
        nc.sync.dma_start(out=eps_raw[:], in_=eps.rearrange("(p i) d -> p i d", i=TILES))

        stats = [keep.tile([P, 21], F32, name="stats%d" % w) for w in range(2)]
        stats_z = keep.tile([P, 15], F32, name="stats_z")
        for st in (stats[0], stats[1], stats_z):
            n = st.shape[1]
            nc.vector.memset(st[:, n - 3 : n - 1], 0.0)
            nc.vector.memset(st[:, n - 1 : n], ROWS * BN_EPS)
        warm = keep.tile([P, 1], F32, name="warm")
        nc.vector.memset(warm[:], 0.0)
        warm_out = keep.tile([P, 1], F32, name="warm_out")
        nc.scalar.activation(out=warm_out[:], in_=warm[:], func=ACT.Exp)
        ident_f = keep.tile([P, P], F32, name="ident_f")
        make_identity(nc, ident_f[:])
        ident_b = keep.tile([P, P], BF16, name="ident_b")
        make_identity(nc, ident_b[:])
        neg_half = keep.tile([P, 1], F32, name="neg_half")
        nc.gpsimd.memset(neg_half[:], -0.5)

        scale_bc = keep.tile([P, K1], F32, name="scale_bc", align_bytes=64)
        for g in range(PASSES):
            st = psum.tile([P, 4, P], F32, name="xt%d" % g)
            for t in range(4):
                nc.tensor.transpose(st[:, t, :], scale_k[g][:, t : t + 1].to_broadcast([P, P]), ident_f[:])
            copy = (nc.vector.tensor_copy, nc.scalar.copy)[g]
            width = (P // 2, P)[g]
            for m in range(0, P, width):
                copy(
                    out=scale_bc[:, 512 * g + 4 * m : 512 * g + 4 * (m + width)].rearrange("p (m t) -> p m t", t=4),
                    in_=st[:, :, m : m + width].rearrange("p t m -> p m t"),
                )

        prod = {}
        turned = {}
        grouped = {}
        x_codes = {}
        x_planes = {}
        where = {}
        for c, (first, count) in enumerate(CHUNKS):
            for ii in range(count):
                where[first + ii] = (c, ii)

        def product(i, ks=slice(0, K1)):
            if i not in prod:
                t = ring.tile([P, K1], BF16, name="prod", align_bytes=64)
                prod[i] = t
            nc.vector.tensor_tensor(
                out=prod[i][:, ks], in0=x_bytes[i // 2][:, i % 2, ks].bitcast(FP8), in1=scale_bc[:, ks], op=MULT
            )

        def turn(i):
            xt = psum.tile([P, PASSES, 2, P], F32, name=("xt0", "xt1", "head01", "head11")[i % 4])
            turned[i] = xt
            words = prod[i][:].bitcast(F32)
            for g in range(PASSES):
                for u in range(2):
                    nc.tensor.transpose(xt[:, g, u, :], words[:, 256 * g + u : 256 * (g + 1) : 2], ident_f[:])

        def empty(i):
            c, ii = where[i]
            n = CHUNKS[c][1] * P
            if ii == 0:
                gt = ring.tile([P, PASSES, n * 4], BF16, name="gt", align_bytes=64)
                grouped[c] = gt
            dst = grouped[c][:].bitcast(F32)[:, :, 256 * ii : 256 * (ii + 1)]
            nc.scalar.copy(
                out=dst.rearrange("p g (r u) -> p g r u", u=2), in_=turned[i][:].rearrange("p g u r -> p g r u")
            )

        def quant_x(c):
            n = CHUNKS[c][1] * P
            xc = keep.tile([P, PASSES, n], U32, name="xc%d" % c, align_bytes=64)
            xs = keep.tile([P, PASSES, n], U8, name="xs%d" % c, align_bytes=64)
            x_codes[c] = xc
            x_planes[c] = xs
            nc.vector.quantize_mx(
                out=xc[:].rearrange("p g n -> p (g n)").bitcast(FP8X4),
                scales=xs[:].rearrange("p g n -> p (g n)"),
                in_=grouped[c][:].rearrange("p g n -> p (g n)"),
            )

        w_grp = []
        w_codes = []
        w_planes = []
        for g in range(PASSES):
            w_grp.append(keep.tile([P, 4, P, 4], BF16, name="wg%d" % g, align_bytes=64))
            w_codes.append(keep.tile([P, K2], U32, name="wc%d" % g, align_bytes=64))
            w_planes.append(keep.tile([P, K2], U8, name="ws%d" % g, align_bytes=64))

        def weave_w(g, half):
            ms = slice(64 * half, 64 * half + 64)
            nc.scalar.copy(
                out=w_grp[g][:].rearrange("p t m j -> p m j t")[:, ms, :, :],
                in_=w_raw[g][:].rearrange("p j (m t) -> p m j t", t=4)[:, ms, :, :],
            )

        def quant_w(g):
            nc.vector.quantize_mx(
                out=w_codes[g][:].bitcast(FP8X4),
                scales=w_planes[g][:],
                in_=w_grp[g][:].rearrange("p t m j -> p (t m j)"),
            )

        l_grp = keep.tile([P, 2, D, 4], BF16, name="l_grp", align_bytes=64)
        l_codes = keep.tile([P, 2 * D], U32, name="l_codes", align_bytes=64)
        l_planes = keep.tile([P, 2 * D], U8, name="l_planes", align_bytes=64)

        def weave_l(w):
            nc.scalar.copy(
                out=l_grp[:, w, :, :].rearrange("p (c i) j -> p c j i", i=4),
                in_=l_raw[:, w, :, :].rearrange("p j (c i) -> p c j i", i=4),
            )

        def quant_l():
            nc.vector.quantize_mx(
                out=l_codes[:].bitcast(FP8X4), scales=l_planes[:], in_=l_grp[:].rearrange("p w n j -> p (w n j)")
            )

        acc = {}

        def mm1(c, pair):
            n = CHUNKS[c][1] * P
            if c in ADDED:
                a = psum.tile([P, 4, n], F32, name=("xt1", "acc0")[c - 3])
            else:
                a = psum.tile([P, 2, n], F32, name="acc%d" % pair)
            if True:
                acc[c, pair] = a
                for tt in range(4 if c in ADDED else 2):
                    cols = slice(P * (2 * pair + tt), P * (2 * pair + tt) + P)
                    for g in range(PASSES):
                        nc.tensor.matmul_mx(
                            out=a[:, tt, :],
                            lhsT=w_codes[g][:, cols].bitcast(FP8X4),
                            lhsT_scale=w_planes[g][:, cols],
                            rhs=x_codes[c][:, g, :].bitcast(FP8X4),
                            rhs_scale=x_planes[c][:, g, :],
                            start=(g == 0),
                            stop=(g == PASSES - 1),
                        )

        hidden = {}
        h_grp = {}

        def relu(c, ts):
            n = CHUNKS[c][1] * P
            if c not in hidden:
                h = ring.tile([P, 4, n], BF16, name="hid", align_bytes=64)
                hidden[c] = h
            for t in ts:
                nc.scalar.activation(
                    out=hidden[c][:, t, :], in_=acc[c, t // 2][:, t % 2, :], func=ACT.Relu, bias=b2_raw[:, t : t + 1]
                )

        def add_b2(c):
            hg = ring.tile([P, P, 4], BF16, name="hg", align_bytes=64)
            h_grp[c] = hg
            nc.vector.tensor_tensor(
                out=hg[:],
                in0=acc[c, 0][:].rearrange("p t n -> p n t"),
                in1=b2_raw[:].unsqueeze(1).to_broadcast([P, P, 4]),
                op=ADD,
            )

        def relu_in_place(c):
            if c == 3:
                nc.scalar.activation(out=h_grp[c][:], in_=h_grp[c][:], func=ACT.Relu)
            else:
                nc.vector.tensor_scalar(
                    out=h_grp[c][:], in0=h_grp[c][:], scalar1=0.0, scalar2=None, op0=mybir.AluOpType.max
                )

        h_codes = {}
        h_planes = {}

        def weave_h(c):
            n = CHUNKS[c][1] * P
            hg = ring.tile([P, n, 4], BF16, name="hg", align_bytes=64)
            h_grp[c] = hg
            dst = hg[:].rearrange("p (c i) t -> p c t i", i=4)
            src = hidden[c][:].rearrange("p t (c i) -> p c t i", i=4)
            if c == 2:
                nc.scalar.copy(out=dst, in_=src)
            else:
                nc.vector.tensor_copy(out=dst, in_=src)

        def quant_h(c):
            n = CHUNKS[c][1] * P
            hc = ring.tile([P, n], U32, name="hc", align_bytes=64)
            hs = ring.tile([P, n], U8, name="hs", align_bytes=64)
            h_codes[c] = hc
            h_planes[c] = hs
            nc.vector.quantize_mx(
                out=hc[:].bitcast(FP8X4), scales=hs[:], in_=h_grp[c][:].rearrange("p n t -> p (n t)")
            )

        heads = [{}, {}]

        def place(c):
            first, count = CHUNKS[c]
            return first // 4, slice((first % 4) * P, (first % 4 + count) * P)

        def mm2(c):
            h, cols = place(c)
            for w in (1, 0):
                if h not in heads[w]:
                    head = psum.tile([P, 512], F32, name="head%d%d" % (w, h))
                    heads[w][h] = head
                nc.tensor.matmul_mx(
                    out=heads[w][h][:, cols],
                    lhsT=l_codes[:, D * w : D * w + D].bitcast(FP8X4),
                    lhsT_scale=l_planes[:, D * w : D * w + D],
                    rhs=h_codes[c][:].bitcast(FP8X4),
                    rhs_scale=h_planes[c][:],
                    start=True,
                    stop=True,
                )

        def stat(part, ws=(1, 0)):
            h, cols = ((0, slice(0, 512)), (1, slice(0, 384)), (1, slice(384, 512)))[part]
            for w in ws:
                nc.vector.bn_stats(out=stats[w][:, 6 * part : 6 * part + 6], in_=heads[w][h][:, cols])

        eps_bank = []

        def turn_eps():
            et = psum.tile([P, TILES, P], BF16, name="xt0")
            for i in range(TILES):
                nc.tensor.transpose(et[:, i, :], eps_raw[:, i, :], ident_b[:])
            eps_bank.append(et)

        product(0, slice(0, 256))
        product(0, slice(256, 512))
        weave_w(0, 0)
        product(1, slice(0, 512))
        product(0, slice(512, K1))
        weave_w(0, 1)
        product(1, slice(512, K1))
        turn(0)
        product(2)
        turn(1)
        weave_w(1, 0)
        product(3)
        turn(2)
        empty(0)
        empty(1)
        product(4)
        turn(3)
        weave_w(1, 1)
        quant_w(0)
        turn(4)
        weave_l(0)
        quant_x(0)
        empty(2)
        quant_w(1)
        empty(3)
        product(5)
        mm1(0, 0)
        empty(4)
        mm1(0, 1)
        relu(0, (1,))
        quant_x(1)
        relu(0, (0,))
        turn(5)
        relu(0, (2,))
        product(6)
        mm1(1, 0)
        relu(0, (3,))
        weave_l(1)
        mm1(1, 1)
        product(7)
        empty(5)
        turn(6)
        relu(1, (0,))
        relu(1, (2,))
        quant_x(2)
        relu(1, (1,))
        turn(7)
        relu(1, (3,))
        weave_h(0)
        empty(6)
        mm1(2, 0)
        quant_l()
        empty(7)
        mm1(2, 1)
        quant_x(3)
        relu(2, (1,))
        quant_h(0)
        mm1(3, 0)
        relu(2, (0,))
        quant_x(4)
        relu(2, (2,))
        weave_h(1)
        mm1(4, 0)
        relu(2, (3,))
        add_b2(3)
        weave_h(2)
        mm2(0)
        turn_eps()
        add_b2(4)
        quant_h(1)
        relu_in_place(3)
        relu_in_place(4)
        mm2(1)
        quant_h(2)
        quant_h(4)
        mm2(2)
        quant_h(3)
        mm2(4)
        mm2(3)

        mv = [keep.tile([P, 2], F32, name="mv%d" % w) for w in range(2)]
        rs = [keep.tile([P, 1], F32, name="rs%d" % w) for w in range(2)]
        nb = [keep.tile([P, 1], F32, name="nb%d" % w) for w in range(2)]
        half_rs = keep.tile([P, 1], F32, name="half_rs")
        half_nm = keep.tile([P, 1], F32, name="half_nm")
        dev = keep.tile([P, 2, 512], F32, name="dev", align_bytes=64)
        for part in (0, 2, 1):
            stat(part, (1,))
        nc.vector.bn_aggr(out=mv[1][:], in_=stats[1][:])
        nc.gpsimd.tensor_tensor(out=rs[1][:], in0=mv[1][:, 1:2], in1=neg_half[:], op=POW)
        nc.vector.tensor_scalar(out=half_nm[:], in0=mv[1][:, 0:1], scalar1=-0.5, scalar2=None, op0=MULT)
        nc.scalar.activation(out=dev[:, 0, :], in_=heads[1][0][:], func=ACT.Identity, bias=half_nm[:], scale=0.5)
        for part in range(3):
            stat(part, (0,))
        nc.vector.scalar_tensor_tensor(
            out=nb[1][:], in0=mv[1][:, 0:1], scalar=-0.5, in1=rs[1][:], op0=MULT, op1=MULT
        )
        nc.vector.tensor_scalar(out=half_rs[:], in0=rs[1][:], scalar1=0.5, scalar2=None, op0=MULT)
        nc.vector.bn_aggr(out=mv[0][:], in_=stats[0][:])
        nc.gpsimd.tensor_tensor(out=rs[0][:], in0=mv[0][:, 1:2], in1=neg_half[:], op=POW)

        noise = keep.tile([P, 2, 512], F32, name="noise", align_bytes=64)
        z_t = keep.tile([P, 2, 512], F32, name="z_t", align_bytes=64)
        zf_t = keep.tile([P, 2, 512], F32, name="zf_t", align_bytes=64)
        zx_t = keep.tile([P, 2, 512], F32, name="zx_t", align_bytes=64)
        def turn_back(src, h, part, name):
            b = psum.tile([P, 2, P], F32, name=name)
            for i in range(2):
                nc.tensor.transpose(b[:, i, :], src[:, h, part.start + P * i : part.start + P * i + P], ident_f[:])
            return b

        quarters = [(q // 2, slice(256 * (q % 2), 256 * (q % 2) + 256)) for q in range(4)]
        for h, part in quarters:
            if h == 0:
                nc.scalar.activation(out=dev[:, h, part], in_=dev[:, h, part], func=ACT.Exp, scale=rs[1][:])
            else:
                nc.scalar.activation(
                    out=dev[:, h, part], in_=heads[1][h][:, part], func=ACT.Exp, bias=nb[1][:], scale=half_rs[:]
                )
        nc.scalar.activation(out=warm_out[:], in_=mv[1][:, 1:2], func=ACT.Abs_reciprocal_sqrt)
        for q, (h, part) in enumerate(quarters):
            nc.vector.tensor_tensor(
                out=noise[:, h, part],
                in0=dev[:, h, part],
                in1=eps_bank[0][:, 2 * q : 2 * q + 2, :].rearrange("p i r -> p (i r)"),
                op=MULT,
            )
        nc.vector.scalar_tensor_tensor(
            out=nb[0][:], in0=mv[0][:, 0:1], scalar=-1.0, in1=rs[0][:], op0=MULT, op1=MULT
        )
        for h, part in quarters:
            nc.vector.scalar_tensor_tensor(
                out=z_t[:, h, part], in0=heads[0][h][:, part], scalar=rs[0][:], in1=noise[:, h, part], op0=MULT, op1=ADD
            )
        z_bank = []
        for h in range(2):
            nc.vector.bn_stats(out=stats_z[:, 6 * h : 6 * h + 6], in_=z_t[:, h, :])
        for q, (h, part) in enumerate(quarters):
            nc.scalar.activation(out=zf_t[:, h, part], in_=z_t[:, h, part], func=ACT.Identity, bias=nb[0][:])
            z_bank.append(turn_back(zf_t, h, part, ("xt1", "acc0", "acc1", "head10")[q]))
        mvz = keep.tile([P, 2], F32, name="mvz")
        rsz = keep.tile([P, 1], F32, name="rsz")
        nc.vector.bn_aggr(out=mvz[:], in_=stats_z[:])
        z_out = keep.tile([P, TILES, P], F32, name="z_out", align_bytes=64)
        zx_out = keep.tile([P, TILES, P], F32, name="zx_out", align_bytes=64)
        z_rows = out_z.rearrange("(p i) d -> p i d", i=TILES)
        zx_rows = out_zx.rearrange("(p i) d -> p i d", i=TILES)
        for q in range(4):
            if q == 2:
                nc.scalar.activation(out=rsz[:], in_=mvz[:, 1:2], func=ACT.Abs_reciprocal_sqrt)
            nc.scalar.copy(out=z_out[:, 2 * q : 2 * q + 2, :], in_=z_bank[q][:])
            if q % 2 == 1:
                nc.sync.dma_start(out=z_rows[:, 2 * q - 2 : 2 * q + 2, :], in_=z_out[:, 2 * q - 2 : 2 * q + 2, :])
        zx_bank = []
        for q, (h, part) in enumerate(quarters):
            nc.vector.tensor_scalar(
                out=zx_t[:, h, part], in0=z_t[:, h, part], scalar1=mvz[:, 0:1], scalar2=rsz[:], op0=SUB, op1=MULT
            )
            zx_bank.append(turn_back(zx_t, h, part, ("head11", "xt0", "xt1", "acc0")[q]))
        for q in range(4):
            cols = slice(2 * q, 2 * q + 2)
            copy = (nc.scalar.copy, nc.vector.tensor_copy)[q % 2]
            copy(out=zx_out[:, cols, :], in_=zx_bank[q][:])
            nc.sync.dma_start(out=zx_rows[:, cols, :], in_=zx_out[:, cols, :])
